import numpy as np
import ml_dtypes


def mxq(x, axis, fmt="e4m3"):
    dtype, down = {"e4m3": (ml_dtypes.float8_e4m3fn, 7), "e5m2": (ml_dtypes.float8_e5m2, 14)}[fmt]
    v = np.moveaxis(np.asarray(x, np.float32).astype(ml_dtypes.bfloat16).astype(np.float64), axis, -1)
    blocks = v.reshape(v.shape[:-1] + (-1, 32))
    amax = np.abs(blocks).max(-1, keepdims=True)
    byte = np.maximum(np.where(amax > 0, np.frexp(amax)[1] - 1 + 127, 0) - down, 1)
    scale = np.exp2(byte - 127.0)
    codes = (blocks / scale).astype(np.float32).astype(dtype).astype(np.float64)
    return np.moveaxis((codes * scale).reshape(v.shape), -1, axis)


WIDE = False


def mx_kscale(k):
    if not WIDE:
        return np.ones(k)
    levels = np.array([10, -10, 5, -5, 0])
    a = np.random.permutation(np.resize(levels, k // 512 * 4)).reshape(k // 512, 4)
    idx = np.arange(k)
    return np.exp2(a[idx // 512, idx % 128 // 32])


BF16 = ml_dtypes.bfloat16


def bf(x):
    return np.asarray(x, np.float32).astype(BF16)


def f64(x):
    return np.asarray(x).astype(np.float64)


B, N, NODE_IN, EDGE_IN, EDGE_OUT = 2, 64, 192, 128, 512
D_IN = 2 * NODE_IN + EDGE_IN
HID = 2 * EDGE_OUT
NEG_SLOPE = 0.1


def leaky_relu(v):
    return np.where(v >= 0.0, v, NEG_SLOPE * v)


def setup_inputs():
    s = mx_kscale(D_IN)
    sn, se = s[:NODE_IN], s[2 * NODE_IN:]
    st = np.concatenate([sn, sn, se])
    return {"node_fts": bf(np.random.standard_normal((B, N, NODE_IN)) * sn),
            "edge_fts": bf(np.random.standard_normal((B, N * N, EDGE_IN)) * se),
            "Wt": bf(np.random.standard_normal((HID, D_IN)) / np.sqrt(D_IN) / st)}


def reference(node_fts, edge_fts, Wt):
    node = f64(node_fts)
    src = np.repeat(node, N, axis=1)
    dst = np.tile(node, (1, N, 1))
    triplet = np.concatenate([src, dst, f64(edge_fts)], axis=-1)
    return leaky_relu(mxq(triplet, 2, "e4m3") @ mxq(f64(Wt).T, 0, "e4m3"))

@@ -1,0 +1,193 @@
+from contextlib import ExitStack
+
+import concourse.mybir as mybir
+from concourse.masks import make_identity
+
+F32 = mybir.dt.float32
+BF16 = mybir.dt.bfloat16
+U32 = mybir.dt.uint32
+U8 = mybir.dt.uint8
+FP8X4 = mybir.dt.float8_e4m3fn_x4
+ALU = mybir.AluOpType
+
+P = 128
+N_NODE = 64
+NODE_IN = 192
+EDGE_IN = 128
+D_IN = 512
+HID = 1024
+HALF = 512
+GT = 4
+N_GROUPS = N_NODE // GT
+CHUNK = 8
+PAD = 3
+N_SLOTS = 4
+NEG_SLOPE = 0.1
+
+FLOPS = 2 * 2 * N_NODE * N_NODE * D_IN * HID
+
+
+def tile_edge_update_only_pa_t_kernel(tc, node_fts, edge_fts, Wt, out):
+    nc = tc.nc
+    edge_v = edge_fts.rearrange("b (i k) f -> (b i) k f", k=N_NODE)
+    out_v = out.rearrange("b (i k) h -> (b i) k h", k=N_NODE)
+    node_rows = node_fts.flatten_outer_dims()
+    w_v = Wt.rearrange("(r p) k -> p r k", p=P)
+
+    with ExitStack() as ctx:
+        const = ctx.enter_context(tc.tile_pool(name="const", bufs=1))
+        qpool = ctx.enter_context(tc.tile_pool(name="qpool", bufs=3))
+        ypool = ctx.enter_context(tc.tile_pool(name="ypool", bufs=4))
+        opool = ctx.enter_context(tc.tile_pool(name="opool", bufs=4))
+        tpp = ctx.enter_context(tc.psum_pool(name="tpp", bufs=2))
+        mxp = ctx.enter_context(tc.psum_pool(name="mxp", bufs=6))
+
+        ident = const.tile([P, P], F32, name="ident")
+        make_identity(nc, ident[:])
+
+        nr = const.tile([P, D_IN], BF16, name="nr")
+        nc.sync.dma_start(out=nr[:, 0:NODE_IN], in_=node_rows)
+        nc.sync.dma_start(out=nr[:, NODE_IN : 2 * NODE_IN], in_=node_rows)
+        nc.vector.memset(nr[:, 2 * NODE_IN : D_IN], 0.0)
+
+        chunks = []
+        for c in range(N_NODE // CHUNK):
+            ec = const.tile([P, (PAD + CHUNK) * EDGE_IN], BF16, name="ec%d" % c)
+            chunks.append(ec)
+
+        def load_chunk(c):
+            ec = chunks[c]
+            if c == 0:
+                nc.vector.memset(ec[:, 0 : PAD * EDGE_IN], 0.0)
+                nc.sync.dma_start(
+                    out=ec[:, PAD * EDGE_IN :].rearrange("p (k f) -> p k f", f=EDGE_IN),
+                    in_=edge_v[:, 0:CHUNK, :],
+                )
+            else:
+                nc.sync.dma_start(
+                    out=ec[:].rearrange("p (k f) -> p k f", f=EDGE_IN),
+                    in_=edge_v[:, c * CHUNK - PAD : (c + 1) * CHUNK, :],
+                )
+
+        load_chunk(0)
+        wsb = const.tile([P, 8 * D_IN], BF16, name="wsb")
+        wsb3 = wsb[:].rearrange("p (r k) -> p r k", r=8)
+        nc.sync.dma_start(out=wsb3[:, :, 0:NODE_IN], in_=w_v[:, :, NODE_IN : 2 * NODE_IN])
+        nc.sync.dma_start(out=wsb3[:, :, NODE_IN : 2 * NODE_IN], in_=w_v[:, :, 0:NODE_IN])
+        nc.sync.dma_start(out=wsb3[:, :, 2 * NODE_IN :], in_=w_v[:, :, 2 * NODE_IN :])
+        for c in range(1, N_NODE // CHUNK):
+            load_chunk(c)
+
+        ntp = tpp.tile([P, 512], F32, tag="tp")
+        nrw = nr[:].bitcast(F32).rearrange("p (m e) -> p m e", e=2)
+        for e in range(2):
+            nc.tensor.transpose(ntp[:, e * P : (e + 1) * P], nrw[:, :, e], ident[:])
+        ntb = const.tile([P, 4 * P], BF16, name="ntb", align_bytes=64)
+        nc.vector.tensor_copy(
+            out=ntb[:].bitcast(F32).rearrange("p (q e) -> p q e", e=2),
+            in_=ntp[:, 0 : 2 * P].rearrange("p (e q) -> p q e", e=2),
+        )
+
+        slots = []
+        for s in range(N_SLOTS):
+            st = const.tile([P, GT * 4 * P], BF16, name="st%d" % s, align_bytes=64)
+            slots.append(st)
+            nc.vector.tensor_copy(
+                out=st[:].rearrange("p (t c) -> p t c", t=GT),
+                in_=ntb[:].unsqueeze(1).to_broadcast([P, GT, 4 * P]),
+            )
+
+        def prep(g):
+            st = slots[g % N_SLOTS]
+            ew = chunks[(g * GT) // CHUNK][:].bitcast(F32)
+            stw = st[:].bitcast(F32).rearrange("p (t q e) -> p t q e", t=GT, e=2)
+            for b in range(2):
+                nc.gpsimd.tensor_scalar(
+                    out=st[0:48, :].rearrange("p (t b i j) -> p t b i j", t=GT, b=2, j=4)[:, :, b, :, :],
+                    in0=ntb[0:48, :]
+                    .rearrange("p (b k j) -> p b k j", b=2, j=4)[:, b, g * GT : (g + 1) * GT, :]
+                    .unsqueeze(2)
+                    .to_broadcast([48, GT, N_NODE, 4]),
+                    scalar1=1.0,
+                    scalar2=0.0,
+                    op0=ALU.mult,
+                    op1=ALU.add,
+                )
+            for pair in range(GT // 2):
+                etp = tpp.tile([P, 512], F32, tag="tp")
+                for tl in range(2):
+                    lt = (g * GT) % CHUNK + pair * 2 + tl
+                    win = ew[:, lt * 64 : lt * 64 + 256].rearrange("p (m e) -> p m e", e=2)
+                    for e in range(2):
+                        col = (tl * 2 + e) * P
+                        nc.tensor.transpose(etp[:, col : col + P], win[:, :, e], ident[:])
+                nc.scalar.copy(
+                    out=stw[96:128, pair * 2 : pair * 2 + 2, :, :],
+                    in_=etp[96:128, :].rearrange("p (t e q) -> p t q e", t=2, e=2),
+                )
+
+        def quantise(g):
+            tq = qpool.tile([P, GT * P], U32, tag="tq", align_bytes=64)
+            ts = qpool.tile([P, GT * P], U8, tag="ts", align_bytes=64)
+            nc.vector.quantize_mx(out=tq[:].bitcast(FP8X4), scales=ts[:], in_=slots[g % N_SLOTS][:])
+            return tq, ts
+
+        prep(0)
+
+        wsw = wsb[:].bitcast(F32).rearrange("p (r m e) -> p r m e", r=8, e=2)
+        wg = const.tile([P, 4 * HID], BF16, name="wg", align_bytes=64)
+        wgw = wg[:].bitcast(F32).rearrange("p (h e) -> p h e", e=2)
+        wq = const.tile([P, HID], U32, name="wq", align_bytes=64)
+        wsc = const.tile([P, HID], U8, name="wsc", align_bytes=64)
+        for rp in range(4):
+            wtp = tpp.tile([P, 512], F32, tag="tp")
+            for rl in range(2):
+                for e in range(2):
+                    col = (rl * 2 + e) * P
+                    nc.tensor.transpose(wtp[:, col : col + P], wsw[:, rp * 2 + rl, :, e], ident[:])
+            dst = wgw[:, rp * 256 : (rp + 1) * 256, :].rearrange("p (r q) e -> p r q e", r=2)
+            src = wtp[:].rearrange("p (r e q) -> p r q e", r=2, e=2)
+            if rp % 2 == 0:
+                nc.vector.tensor_copy(out=dst, in_=src)
+            else:
+                nc.scalar.copy(out=dst, in_=src)
+            if rp % 2 == 1:
+                hf = rp // 2
+                nc.vector.quantize_mx(
+                    out=wq[:, hf * HALF : (hf + 1) * HALF].bitcast(FP8X4),
+                    scales=wsc[:, hf * HALF : (hf + 1) * HALF],
+                    in_=wg[:, hf * 4 * HALF : (hf + 1) * 4 * HALF],
+                )
+
+        def multiply(g, tq, ts):
+            o = opool.tile([P, GT * HID], F32, tag="o")
+            for t in range(GT):
+                for hf in range(2):
+                    mx = mxp.tile([P, HALF], F32, tag="mx")
+                    nc.tensor.matmul_mx(
+                        out=mx[:],
+                        lhsT=tq[:, t * P : (t + 1) * P].bitcast(FP8X4),
+                        lhsT_scale=ts[:, t * P : (t + 1) * P],
+                        rhs=wq[:, hf * HALF : (hf + 1) * HALF].bitcast(FP8X4),
+                        rhs_scale=wsc[:, hf * HALF : (hf + 1) * HALF],
+                        start=True,
+                        stop=True,
+                    )
+                    y = ypool.tile([P, HALF], F32, tag="y")
+                    nc.scalar.mul(out=y[:], in_=mx[:], mul=NEG_SLOPE)
+                    col = t * HID + hf * HALF
+                    nc.vector.tensor_tensor(out=o[:, col : col + HALF], in0=mx[:], in1=y[:], op=ALU.max)
+            nc.sync.dma_start(
+                out=out_v[:, g * GT : (g + 1) * GT, :],
+                in_=o[:].rearrange("p (t h) -> p t h", t=GT),
+            )
+
+        prep(1)
+        ready = {0: quantise(0)}
+        for g in range(N_GROUPS):
+            if g + 2 < N_GROUPS:
+                prep(g + 2)
+            if g + 1 < N_GROUPS:
+                ready[g + 1] = quantise(g + 1)
+            tq, ts = ready[g]
+            multiply(g, tq, ts)

@@ -19,10 +19,11 @@ HID = 1024
 HALF = 512
 GT = 4
 N_GROUPS = N_NODE // GT
-CHUNK = 8
-PAD = 3
-N_SLOTS = 4
+CH = 8
+N_CHUNKS = N_NODE // CH
+N_SLOTS = 3
 NEG_SLOPE = 0.1
+TILE_COLS = 4 * P
 
 FLOPS = 2 * 2 * N_NODE * N_NODE * D_IN * HID
 
@@ -36,6 +37,7 @@ def tile_edge_update_only_pa_t_kernel(tc, node_fts, edge_fts, Wt, out):
 
     with ExitStack() as ctx:
         const = ctx.enter_context(tc.tile_pool(name="const", bufs=1))
+        pkpool = ctx.enter_context(tc.tile_pool(name="pkpool", bufs=3))
         qpool = ctx.enter_context(tc.tile_pool(name="qpool", bufs=3))
         ypool = ctx.enter_context(tc.tile_pool(name="ypool", bufs=4))
         opool = ctx.enter_context(tc.tile_pool(name="opool", bufs=4))
@@ -51,23 +53,15 @@ def tile_edge_update_only_pa_t_kernel(tc, node_fts, edge_fts, Wt, out):
         nc.vector.memset(nr[:, 2 * NODE_IN : D_IN], 0.0)
 
         chunks = []
-        for c in range(N_NODE // CHUNK):
-            ec = const.tile([P, (PAD + CHUNK) * EDGE_IN], BF16, name="ec%d" % c)
+        for c in range(N_CHUNKS):
+            ec = const.tile([P, CH * EDGE_IN], BF16, name="ec%d" % c)
             chunks.append(ec)
 
         def load_chunk(c):
-            ec = chunks[c]
-            if c == 0:
-                nc.vector.memset(ec[:, 0 : PAD * EDGE_IN], 0.0)
-                nc.sync.dma_start(
-                    out=ec[:, PAD * EDGE_IN :].rearrange("p (k f) -> p k f", f=EDGE_IN),
-                    in_=edge_v[:, 0:CHUNK, :],
-                )
-            else:
-                nc.sync.dma_start(
-                    out=ec[:].rearrange("p (k f) -> p k f", f=EDGE_IN),
-                    in_=edge_v[:, c * CHUNK - PAD : (c + 1) * CHUNK, :],
-                )
+            nc.sync.dma_start(
+                out=chunks[c][:].rearrange("p (k f) -> p k f", f=EDGE_IN),
+                in_=edge_v[:, c * CH : (c + 1) * CH, :],
+            )
 
         load_chunk(0)
         wsb = const.tile([P, 8 * D_IN], BF16, name="wsb")
@@ -75,14 +69,14 @@ def tile_edge_update_only_pa_t_kernel(tc, node_fts, edge_fts, Wt, out):
         nc.sync.dma_start(out=wsb3[:, :, 0:NODE_IN], in_=w_v[:, :, NODE_IN : 2 * NODE_IN])
         nc.sync.dma_start(out=wsb3[:, :, NODE_IN : 2 * NODE_IN], in_=w_v[:, :, 0:NODE_IN])
         nc.sync.dma_start(out=wsb3[:, :, 2 * NODE_IN :], in_=w_v[:, :, 2 * NODE_IN :])
-        for c in range(1, N_NODE // CHUNK):
+        for c in range(1, N_CHUNKS):
             load_chunk(c)
 
         ntp = tpp.tile([P, 512], F32, tag="tp")
         nrw = nr[:].bitcast(F32).rearrange("p (m e) -> p m e", e=2)
         for e in range(2):
             nc.tensor.transpose(ntp[:, e * P : (e + 1) * P], nrw[:, :, e], ident[:])
-        ntb = const.tile([P, 4 * P], BF16, name="ntb", align_bytes=64)
+        ntb = const.tile([P, TILE_COLS], BF16, name="ntb", align_bytes=64)
         nc.vector.tensor_copy(
             out=ntb[:].bitcast(F32).rearrange("p (q e) -> p q e", e=2),
             in_=ntp[:, 0 : 2 * P].rearrange("p (e q) -> p q e", e=2),
@@ -90,46 +84,55 @@ def tile_edge_update_only_pa_t_kernel(tc, node_fts, edge_fts, Wt, out):
 
         slots = []
         for s in range(N_SLOTS):
-            st = const.tile([P, GT * 4 * P], BF16, name="st%d" % s, align_bytes=64)
+            st = const.tile([P, CH * TILE_COLS], BF16, name="st%d" % s, align_bytes=64)
             slots.append(st)
             nc.vector.tensor_copy(
-                out=st[:].rearrange("p (t c) -> p t c", t=GT),
-                in_=ntb[:].unsqueeze(1).to_broadcast([P, GT, 4 * P]),
+                out=st[:].rearrange("p (t c) -> p t c", t=CH),
+                in_=ntb[:].unsqueeze(1).to_broadcast([P, CH, TILE_COLS]),
             )
 
-        def prep(g):
-            st = slots[g % N_SLOTS]
-            ew = chunks[(g * GT) // CHUNK][:].bitcast(F32)
-            stw = st[:].bitcast(F32).rearrange("p (t q e) -> p t q e", t=GT, e=2)
-            for b in range(2):
-                nc.gpsimd.tensor_scalar(
-                    out=st[0:48, :].rearrange("p (t b i j) -> p t b i j", t=GT, b=2, j=4)[:, :, b, :, :],
-                    in0=ntb[0:48, :]
-                    .rearrange("p (b k j) -> p b k j", b=2, j=4)[:, b, g * GT : (g + 1) * GT, :]
-                    .unsqueeze(2)
-                    .to_broadcast([48, GT, N_NODE, 4]),
-                    scalar1=1.0,
-                    scalar2=0.0,
-                    op0=ALU.mult,
-                    op1=ALU.add,
-                )
-            for pair in range(GT // 2):
-                etp = tpp.tile([P, 512], F32, tag="tp")
-                for tl in range(2):
-                    lt = (g * GT) % CHUNK + pair * 2 + tl
-                    win = ew[:, lt * 64 : lt * 64 + 256].rearrange("p (m e) -> p m e", e=2)
-                    for e in range(2):
-                        col = (tl * 2 + e) * P
-                        nc.tensor.transpose(etp[:, col : col + P], win[:, :, e], ident[:])
-                nc.scalar.copy(
-                    out=stw[96:128, pair * 2 : pair * 2 + 2, :, :],
-                    in_=etp[96:128, :].rearrange("p (t e q) -> p t q e", t=2, e=2),
+        def prep(c):
+            st = slots[c % N_SLOTS]
+            ew = chunks[c][:].bitcast(F32)
+            for gl in range(2):
+                for b in range(2):
+                    k0 = c * CH + gl * GT
+                    nc.gpsimd.tensor_scalar(
+                        out=st[0:48, gl * GT * TILE_COLS : (gl + 1) * GT * TILE_COLS].rearrange(
+                            "p (t b i j) -> p t b i j", t=GT, b=2, j=4
+                        )[:, :, b, :, :],
+                        in0=ntb[0:48, :]
+                        .rearrange("p (b k j) -> p b k j", b=2, j=4)[:, b, k0 : k0 + GT, :]
+                        .unsqueeze(2)
+                        .to_broadcast([48, GT, N_NODE, 4]),
+                        scalar1=1.0,
+                        scalar2=0.0,
+                        op0=ALU.mult,
+                        op1=ALU.add,
+                    )
+            etp = tpp.tile([P, 512], F32, tag="tp")
+            for gl in range(2):
+                win = ew[:, gl * 256 : (gl + 1) * 256].rearrange("p (m e) -> p m e", e=2)
+                for e in range(2):
+                    col = (gl * 2 + e) * P
+                    nc.tensor.transpose(etp[:, col : col + P], win[:, :, e], ident[:])
+            pk = pkpool.tile([P, 2 * TILE_COLS], BF16, tag="pk")
+            nc.scalar.copy(
+                out=pk[:].bitcast(F32).rearrange("p (g q e) -> p g q e", g=2, e=2),
+                in_=etp[:].rearrange("p (g e q) -> p g q e", g=2, e=2),
+            )
+            for n in range(4):
+                nc.sync.dma_start(
+                    out=st[96:128, :].rearrange("p (g n c) -> p g n c", g=2, n=4)[:, :, n, :],
+                    in_=pk[32 * n : 32 * n + 32, :].rearrange("p (g c) -> p g c", g=2),
                 )
 
         def quantise(g):
+            st = slots[(g // 2) % N_SLOTS]
             tq = qpool.tile([P, GT * P], U32, tag="tq", align_bytes=64)
             ts = qpool.tile([P, GT * P], U8, tag="ts", align_bytes=64)
-            nc.vector.quantize_mx(out=tq[:].bitcast(FP8X4), scales=ts[:], in_=slots[g % N_SLOTS][:])
+            lo = (g % 2) * GT * TILE_COLS
+            nc.vector.quantize_mx(out=tq[:].bitcast(FP8X4), scales=ts[:], in_=st[:, lo : lo + GT * TILE_COLS])
             return tq, ts
 
         prep(0)
@@ -177,16 +180,19 @@ def tile_edge_update_only_pa_t_kernel(tc, node_fts, edge_fts, Wt, out):
                     nc.scalar.mul(out=y[:], in_=mx[:], mul=NEG_SLOPE)
                     col = t * HID + hf * HALF
                     nc.vector.tensor_tensor(out=o[:, col : col + HALF], in0=mx[:], in1=y[:], op=ALU.max)
-            nc.sync.dma_start(
-                out=out_v[:, g * GT : (g + 1) * GT, :],
-                in_=o[:].rearrange("p (t h) -> p t h", t=GT),
-            )
+                if g == N_GROUPS - 1:
+                    nc.sync.dma_start(out=out_v[:, g * GT + t, :], in_=o[:, t * HID : (t + 1) * HID])
+            if g < N_GROUPS - 1:
+                nc.sync.dma_start(
+                    out=out_v[:, g * GT : (g + 1) * GT, :],
+                    in_=o[:].rearrange("p (t h) -> p t h", t=GT),
+                )
 
         prep(1)
         ready = {0: quantise(0)}
         for g in range(N_GROUPS):
-            if g + 2 < N_GROUPS:
-                prep(g + 2)
+            if g % 2 == 0 and g // 2 + 2 < N_CHUNKS:
+                prep(g // 2 + 2)
             if g + 1 < N_GROUPS:
                 ready[g + 1] = quantise(g + 1)
             tq, ts = ready[g]

@@ -43,6 +43,7 @@ def tile_edge_update_only_pa_t_kernel(tc, node_fts, edge_fts, Wt, out):
         opool = ctx.enter_context(tc.tile_pool(name="opool", bufs=4))
         tpp = ctx.enter_context(tc.psum_pool(name="tpp", bufs=2))
         mxp = ctx.enter_context(tc.psum_pool(name="mxp", bufs=6))
+        ctx.enter_context(tc.manual_schedule())
 
         ident = const.tile([P, P], F32, name="ident")
         make_identity(nc, ident[:])
@@ -66,11 +67,11 @@ def tile_edge_update_only_pa_t_kernel(tc, node_fts, edge_fts, Wt, out):
         load_chunk(0)
         wsb = const.tile([P, 8 * D_IN], BF16, name="wsb")
         wsb3 = wsb[:].rearrange("p (r k) -> p r k", r=8)
-        nc.sync.dma_start(out=wsb3[:, :, 0:NODE_IN], in_=w_v[:, :, NODE_IN : 2 * NODE_IN])
-        nc.sync.dma_start(out=wsb3[:, :, NODE_IN : 2 * NODE_IN], in_=w_v[:, :, 0:NODE_IN])
-        nc.sync.dma_start(out=wsb3[:, :, 2 * NODE_IN :], in_=w_v[:, :, 2 * NODE_IN :])
-        for c in range(1, N_CHUNKS):
-            load_chunk(c)
+        for hf in range(2):
+            rows = slice(hf * 4, hf * 4 + 4)
+            nc.sync.dma_start(out=wsb3[:, rows, 0:NODE_IN], in_=w_v[:, rows, NODE_IN : 2 * NODE_IN])
+            nc.sync.dma_start(out=wsb3[:, rows, NODE_IN : 2 * NODE_IN], in_=w_v[:, rows, 0:NODE_IN])
+            nc.sync.dma_start(out=wsb3[:, rows, 2 * NODE_IN :], in_=w_v[:, rows, 2 * NODE_IN :])
 
         ntp = tpp.tile([P, 512], F32, tag="tp")
         nrw = nr[:].bitcast(F32).rearrange("p (m e) -> p m e", e=2)
@@ -86,14 +87,15 @@ def tile_edge_update_only_pa_t_kernel(tc, node_fts, edge_fts, Wt, out):
         for s in range(N_SLOTS):
             st = const.tile([P, CH * TILE_COLS], BF16, name="st%d" % s, align_bytes=64)
             slots.append(st)
-            nc.vector.tensor_copy(
-                out=st[:].rearrange("p (t c) -> p t c", t=CH),
-                in_=ntb[:].unsqueeze(1).to_broadcast([P, CH, TILE_COLS]),
+
+        def fill_src(s):
+            nc.sync.dma_start(
+                out=slots[s][48:96, :].rearrange("p (t c) -> p t c", t=CH),
+                in_=ntb[48:96, :].unsqueeze(1).to_broadcast([48, CH, TILE_COLS]),
             )
 
-        def prep(c):
+        def spread_dst(c):
             st = slots[c % N_SLOTS]
-            ew = chunks[c][:].bitcast(F32)
             for gl in range(2):
                 for b in range(2):
                     k0 = c * CH + gl * GT
@@ -110,16 +112,25 @@ def tile_edge_update_only_pa_t_kernel(tc, node_fts, edge_fts, Wt, out):
                         op0=ALU.mult,
                         op1=ALU.add,
                     )
+
+        banks = {}
+
+        def transpose_edges(c):
+            ew = chunks[c][:].bitcast(F32)
             etp = tpp.tile([P, 512], F32, tag="tp")
             for gl in range(2):
                 win = ew[:, gl * 256 : (gl + 1) * 256].rearrange("p (m e) -> p m e", e=2)
                 for e in range(2):
                     col = (gl * 2 + e) * P
                     nc.tensor.transpose(etp[:, col : col + P], win[:, :, e], ident[:])
+            banks[c] = etp
+
+        def move_edges(c):
+            st = slots[c % N_SLOTS]
             pk = pkpool.tile([P, 2 * TILE_COLS], BF16, tag="pk")
             nc.scalar.copy(
                 out=pk[:].bitcast(F32).rearrange("p (g q e) -> p g q e", g=2, e=2),
-                in_=etp[:].rearrange("p (g e q) -> p g q e", g=2, e=2),
+                in_=banks[c][:].rearrange("p (g e q) -> p g q e", g=2, e=2),
             )
             for n in range(4):
                 nc.sync.dma_start(
@@ -127,15 +138,22 @@ def tile_edge_update_only_pa_t_kernel(tc, node_fts, edge_fts, Wt, out):
                     in_=pk[32 * n : 32 * n + 32, :].rearrange("p (g c) -> p g c", g=2),
                 )
 
+        ready = {}
+
         def quantise(g):
             st = slots[(g // 2) % N_SLOTS]
             tq = qpool.tile([P, GT * P], U32, tag="tq", align_bytes=64)
             ts = qpool.tile([P, GT * P], U8, tag="ts", align_bytes=64)
             lo = (g % 2) * GT * TILE_COLS
             nc.vector.quantize_mx(out=tq[:].bitcast(FP8X4), scales=ts[:], in_=st[:, lo : lo + GT * TILE_COLS])
-            return tq, ts
+            ready[g] = (tq, ts)
 
-        prep(0)
+        fill_src(0)
+        spread_dst(0)
+        transpose_edges(0)
+        move_edges(0)
+        load_chunk(1)
+        load_chunk(2)
 
         wsw = wsb[:].bitcast(F32).rearrange("p (r m e) -> p r m e", r=8, e=2)
         wg = const.tile([P, 4 * HID], BF16, name="wg", align_bytes=64)
@@ -143,7 +161,7 @@ def tile_edge_update_only_pa_t_kernel(tc, node_fts, edge_fts, Wt, out):
         wq = const.tile([P, HID], U32, name="wq", align_bytes=64)
         wsc = const.tile([P, HID], U8, name="wsc", align_bytes=64)
         for rp in range(4):
-            wtp = tpp.tile([P, 512], F32, tag="tp")
+            wtp = mxp.tile([P, 512], F32, tag="mx")
             for rl in range(2):
                 for e in range(2):
                     col = (rl * 2 + e) * P
@@ -161,39 +179,50 @@ def tile_edge_update_only_pa_t_kernel(tc, node_fts, edge_fts, Wt, out):
                     scales=wsc[:, hf * HALF : (hf + 1) * HALF],
                     in_=wg[:, hf * 4 * HALF : (hf + 1) * 4 * HALF],
                 )
+        quantise(0)
+        fill_src(1)
+        spread_dst(1)
+        transpose_edges(1)
+        move_edges(1)
+        fill_src(2)
+        load_chunk(3)
 
-        def multiply(g, tq, ts):
+        for g in range(N_GROUPS):
+            c = g // 2
+            tq, ts = ready[g]
             o = opool.tile([P, GT * HID], F32, tag="o")
-            for t in range(GT):
-                for hf in range(2):
-                    mx = mxp.tile([P, HALF], F32, tag="mx")
-                    nc.tensor.matmul_mx(
-                        out=mx[:],
-                        lhsT=tq[:, t * P : (t + 1) * P].bitcast(FP8X4),
-                        lhsT_scale=ts[:, t * P : (t + 1) * P],
-                        rhs=wq[:, hf * HALF : (hf + 1) * HALF].bitcast(FP8X4),
-                        rhs_scale=wsc[:, hf * HALF : (hf + 1) * HALF],
-                        start=True,
-                        stop=True,
-                    )
-                    y = ypool.tile([P, HALF], F32, tag="y")
-                    nc.scalar.mul(out=y[:], in_=mx[:], mul=NEG_SLOPE)
-                    col = t * HID + hf * HALF
-                    nc.vector.tensor_tensor(out=o[:, col : col + HALF], in0=mx[:], in1=y[:], op=ALU.max)
-                if g == N_GROUPS - 1:
-                    nc.sync.dma_start(out=out_v[:, g * GT + t, :], in_=o[:, t * HID : (t + 1) * HID])
+            if g % 2 == 0 and c + 2 < N_CHUNKS:
+                spread_dst(c + 2)
+            if g % 2 == 0 and c + 4 < N_CHUNKS:
+                load_chunk(c + 4)
+            for j in range(2 * GT):
+                t = j // 2
+                hf = j % 2
+                mx = mxp.tile([P, HALF], F32, tag="mx")
+                nc.tensor.matmul_mx(
+                    out=mx[:],
+                    lhsT=tq[:, t * P : (t + 1) * P].bitcast(FP8X4),
+                    lhsT_scale=ts[:, t * P : (t + 1) * P],
+                    rhs=wq[:, hf * HALF : (hf + 1) * HALF].bitcast(FP8X4),
+                    rhs_scale=wsc[:, hf * HALF : (hf + 1) * HALF],
+                    start=True,
+                    stop=True,
+                )
+                y = ypool.tile([P, HALF], F32, tag="y")
+                nc.scalar.mul(out=y[:], in_=mx[:], mul=NEG_SLOPE)
+                col = t * HID + hf * HALF
+                nc.vector.tensor_tensor(out=o[:, col : col + HALF], in0=mx[:], in1=y[:], op=ALU.max)
+                if j == 1 and g + 1 < N_GROUPS:
+                    quantise(g + 1)
+                if j == 1 and g % 2 == 1 and c + 2 < N_CHUNKS:
+                    move_edges(c + 2)
+                if g == N_GROUPS - 1 and (hf == 1 or t == GT - 1):
+                    lo = col if t == GT - 1 else t * HID
+                    nc.sync.dma_start(out=out_v[:, g * GT + t, lo - t * HID : col + HALF - t * HID], in_=o[:, lo : col + HALF])
+            if g % 2 == 0 and c + 2 < N_CHUNKS:
+                transpose_edges(c + 2)
             if g < N_GROUPS - 1:
                 nc.sync.dma_start(
                     out=out_v[:, g * GT : (g + 1) * GT, :],
                     in_=o[:].rearrange("p (t h) -> p t h", t=GT),
                 )
-
-        prep(1)
-        ready = {0: quantise(0)}
-        for g in range(N_GROUPS):
-            if g % 2 == 0 and g // 2 + 2 < N_CHUNKS:
-                prep(g // 2 + 2)
-            if g + 1 < N_GROUPS:
-                ready[g + 1] = quantise(g + 1)
-            tq, ts = ready[g]
-            multiply(g, tq, ts)

@@ -9,6 +9,7 @@ U32 = mybir.dt.uint32
 U8 = mybir.dt.uint8
 FP8X4 = mybir.dt.float8_e4m3fn_x4
 ALU = mybir.AluOpType
+ACT = mybir.ActivationFunctionType
 
 P = 128
 N_NODE = 64
@@ -209,9 +210,16 @@ def tile_edge_update_only_pa_t_kernel(tc, node_fts, edge_fts, Wt, out):
                     stop=True,
                 )
                 y = ypool.tile([P, HALF], F32, tag="y")
-                nc.scalar.mul(out=y[:], in_=mx[:], mul=NEG_SLOPE)
                 col = t * HID + hf * HALF
-                nc.vector.tensor_tensor(out=o[:, col : col + HALF], in0=mx[:], in1=y[:], op=ALU.max)
+                if g % 2 == 1 and j == 2:
+                    nc.scalar.copy(out=o[:, col : col + HALF], in_=mx[:])
+                    nc.scalar.activation(out=y[:], in_=mx[:], func=ACT.Relu, scale=NEG_SLOPE - 1.0)
+                    nc.gpsimd.tensor_tensor(
+                        out=o[:, col : col + HALF], in0=o[:, col : col + HALF], in1=y[:], op=ALU.add
+                    )
+                else:
+                    nc.scalar.mul(out=y[:], in_=mx[:], mul=NEG_SLOPE)
+                    nc.vector.tensor_tensor(out=o[:, col : col + HALF], in0=mx[:], in1=y[:], op=ALU.max)
                 if j == 1 and g + 1 < N_GROUPS:
                     quantise(g + 1)
                 if j == 1 and g % 2 == 1 and c + 2 < N_CHUNKS:

@@ -9,7 +9,6 @@ U32 = mybir.dt.uint32
 U8 = mybir.dt.uint8
 FP8X4 = mybir.dt.float8_e4m3fn_x4
 ALU = mybir.AluOpType
-ACT = mybir.ActivationFunctionType
 
 P = 128
 N_NODE = 64
@@ -153,8 +152,10 @@ def tile_edge_update_only_pa_t_kernel(tc, node_fts, edge_fts, Wt, out):
         spread_dst(0)
         transpose_edges(0)
         move_edges(0)
-        load_chunk(1)
-        load_chunk(2)
+        for c in range(1, N_CHUNKS):
+            load_chunk(c)
+        fill_src(1)
+        fill_src(2)
 
         wsw = wsb[:].bitcast(F32).rearrange("p (r m e) -> p r m e", r=8, e=2)
         wg = const.tile([P, 4 * HID], BF16, name="wg", align_bytes=64)
@@ -169,7 +170,7 @@ def tile_edge_update_only_pa_t_kernel(tc, node_fts, edge_fts, Wt, out):
                     nc.tensor.transpose(wtp[:, col : col + P], wsw[:, rp * 2 + rl, :, e], ident[:])
             dst = wgw[:, rp * 256 : (rp + 1) * 256, :].rearrange("p (r q) e -> p r q e", r=2)
             src = wtp[:].rearrange("p (r e q) -> p r q e", r=2, e=2)
-            if rp % 2 == 0:
+            if rp == 0:
                 nc.vector.tensor_copy(out=dst, in_=src)
             else:
                 nc.scalar.copy(out=dst, in_=src)
@@ -180,22 +181,19 @@ def tile_edge_update_only_pa_t_kernel(tc, node_fts, edge_fts, Wt, out):
                     scales=wsc[:, hf * HALF : (hf + 1) * HALF],
                     in_=wg[:, hf * 4 * HALF : (hf + 1) * 4 * HALF],
                 )
-        quantise(0)
-        fill_src(1)
+            if rp == 1:
+                quantise(0)
         spread_dst(1)
         transpose_edges(1)
         move_edges(1)
-        fill_src(2)
-        load_chunk(3)
 
         for g in range(N_GROUPS):
             c = g // 2
             tq, ts = ready[g]
             o = opool.tile([P, GT * HID], F32, tag="o")
+            per_store = 1 if g == 0 or g >= N_GROUPS - 2 else 2
             if g % 2 == 0 and c + 2 < N_CHUNKS:
                 spread_dst(c + 2)
-            if g % 2 == 0 and c + 4 < N_CHUNKS:
-                load_chunk(c + 4)
             for j in range(2 * GT):
                 t = j // 2
                 hf = j % 2
@@ -210,27 +208,18 @@ def tile_edge_update_only_pa_t_kernel(tc, node_fts, edge_fts, Wt, out):
                     stop=True,
                 )
                 y = ypool.tile([P, HALF], F32, tag="y")
+                nc.scalar.mul(out=y[:], in_=mx[:], mul=NEG_SLOPE)
                 col = t * HID + hf * HALF
-                if g % 2 == 1 and j == 2:
-                    nc.scalar.copy(out=o[:, col : col + HALF], in_=mx[:])
-                    nc.scalar.activation(out=y[:], in_=mx[:], func=ACT.Relu, scale=NEG_SLOPE - 1.0)
-                    nc.gpsimd.tensor_tensor(
-                        out=o[:, col : col + HALF], in0=o[:, col : col + HALF], in1=y[:], op=ALU.add
-                    )
-                else:
-                    nc.scalar.mul(out=y[:], in_=mx[:], mul=NEG_SLOPE)
-                    nc.vector.tensor_tensor(out=o[:, col : col + HALF], in0=mx[:], in1=y[:], op=ALU.max)
+                nc.vector.tensor_tensor(out=o[:, col : col + HALF], in0=mx[:], in1=y[:], op=ALU.max)
                 if j == 1 and g + 1 < N_GROUPS:
                     quantise(g + 1)
                 if j == 1 and g % 2 == 1 and c + 2 < N_CHUNKS:
                     move_edges(c + 2)
-                if g == N_GROUPS - 1 and (hf == 1 or t == GT - 1):
-                    lo = col if t == GT - 1 else t * HID
-                    nc.sync.dma_start(out=out_v[:, g * GT + t, lo - t * HID : col + HALF - t * HID], in_=o[:, lo : col + HALF])
+                if hf == 1 and (t + 1) % per_store == 0:
+                    t0 = t + 1 - per_store
+                    nc.sync.dma_start(
+                        out=out_v[:, g * GT + t0 : g * GT + t + 1, :],
+                        in_=o[:, t0 * HID : (t + 1) * HID].rearrange("p (t h) -> p t h", t=per_store),
+                    )
             if g % 2 == 0 and c + 2 < N_CHUNKS:
                 transpose_edges(c + 2)
-            if g < N_GROUPS - 1:
-                nc.sync.dma_start(
-                    out=out_v[:, g * GT : (g + 1) * GT, :],
-                    in_=o[:].rearrange("p (t h) -> p t h", t=GT),
-                )

@@ -128,7 +128,7 @@ def tile_edge_update_only_pa_t_kernel(tc, node_fts, edge_fts, Wt, out):
         def move_edges(c):
             st = slots[c % N_SLOTS]
             pk = pkpool.tile([P, 2 * TILE_COLS], BF16, tag="pk")
-            nc.scalar.copy(
+            nc.vector.tensor_copy(
                 out=pk[:].bitcast(F32).rearrange("p (g q e) -> p g q e", g=2, e=2),
                 in_=banks[c][:].rearrange("p (g e q) -> p g q e", g=2, e=2),
             )

@@ -22,8 +22,10 @@ N_GROUPS = N_NODE // GT
 CH = 8
 N_CHUNKS = N_NODE // CH
 N_SLOTS = 3
+PAD = 3
 NEG_SLOPE = 0.1
 TILE_COLS = 4 * P
+TILE_WORDS = EDGE_IN // 2
 
 FLOPS = 2 * 2 * N_NODE * N_NODE * D_IN * HID
 
@@ -55,12 +57,15 @@ def tile_edge_update_only_pa_t_kernel(tc, node_fts, edge_fts, Wt, out):
 
         chunks = []
         for c in range(N_CHUNKS):
-            ec = const.tile([P, CH * EDGE_IN], BF16, name="ec%d" % c)
+            lead = PAD if c == 0 else 0
+            ec = const.tile([P, (lead + CH) * EDGE_IN], BF16, name="ec%d" % c)
             chunks.append(ec)
+        nc.vector.memset(chunks[0][:, 0 : PAD * EDGE_IN], 0.0)
 
         def load_chunk(c):
+            lead = PAD if c == 0 else 0
             nc.sync.dma_start(
-                out=chunks[c][:].rearrange("p (k f) -> p k f", f=EDGE_IN),
+                out=chunks[c][:, lead * EDGE_IN :].rearrange("p (k f) -> p k f", f=EDGE_IN),
                 in_=edge_v[:, c * CH : (c + 1) * CH, :],
             )
 
@@ -113,29 +118,51 @@ def tile_edge_update_only_pa_t_kernel(tc, node_fts, edge_fts, Wt, out):
                         op1=ALU.add,
                     )
 
+        def transpose_window(bank, slot, words):
+            win = words.rearrange("p (m e) -> p m e", e=2)
+            for e in range(2):
+                col = (2 * slot + e) * P
+                nc.tensor.transpose(bank[:, col : col + P], win[:, :, e], ident[:])
+
+        def stage_first_group():
+            padded = chunks[0][:].bitcast(F32)
+            stw = slots[0][:].bitcast(F32).rearrange("p (t q e) -> p t q e", t=CH, e=2)
+            for pair in range(GT // 2):
+                bank = tpp.tile([P, 512], F32, tag="tp")
+                for tl in range(2):
+                    t = 2 * pair + tl
+                    transpose_window(bank, tl, padded[:, t * TILE_WORDS : (t + GT) * TILE_WORDS])
+                nc.scalar.copy(
+                    out=stw[96:128, 2 * pair : 2 * pair + 2, :, :],
+                    in_=bank[96:128, :].rearrange("p (t e q) -> p t q e", t=2, e=2),
+                )
+
+        def chunk_groups(c):
+            return range(1, 2) if c == 0 else range(2)
+
         banks = {}
 
         def transpose_edges(c):
-            ew = chunks[c][:].bitcast(F32)
-            etp = tpp.tile([P, 512], F32, tag="tp")
-            for gl in range(2):
-                win = ew[:, gl * 256 : (gl + 1) * 256].rearrange("p (m e) -> p m e", e=2)
-                for e in range(2):
-                    col = (gl * 2 + e) * P
-                    nc.tensor.transpose(etp[:, col : col + P], win[:, :, e], ident[:])
-            banks[c] = etp
+            lead = PAD if c == 0 else 0
+            words = chunks[c][:].bitcast(F32)
+            bank = tpp.tile([P, 512], F32, tag="tp")
+            for gl in chunk_groups(c):
+                w0 = (lead + gl * GT) * TILE_WORDS
+                transpose_window(bank, gl, words[:, w0 : w0 + GT * TILE_WORDS])
+            banks[c] = bank
 
         def move_edges(c):
             st = slots[c % N_SLOTS]
+            groups = slice(chunk_groups(c)[0], 2)
             pk = pkpool.tile([P, 2 * TILE_COLS], BF16, tag="pk")
-            nc.vector.tensor_copy(
-                out=pk[:].bitcast(F32).rearrange("p (g q e) -> p g q e", g=2, e=2),
-                in_=banks[c][:].rearrange("p (g e q) -> p g q e", g=2, e=2),
+            nc.scalar.copy(
+                out=pk[:].bitcast(F32).rearrange("p (g q e) -> p g q e", g=2, e=2)[:, groups, :, :],
+                in_=banks[c][:].rearrange("p (g e q) -> p g q e", g=2, e=2)[:, groups, :, :],
             )
             for n in range(4):
                 nc.sync.dma_start(
-                    out=st[96:128, :].rearrange("p (g n c) -> p g n c", g=2, n=4)[:, :, n, :],
-                    in_=pk[32 * n : 32 * n + 32, :].rearrange("p (g c) -> p g c", g=2),
+                    out=st[96:128, :].rearrange("p (g n c) -> p g n c", g=2, n=4)[:, groups, n, :],
+                    in_=pk[32 * n : 32 * n + 32, :].rearrange("p (g c) -> p g c", g=2)[:, groups, :],
                 )
 
         ready = {}
@@ -148,44 +175,47 @@ def tile_edge_update_only_pa_t_kernel(tc, node_fts, edge_fts, Wt, out):
             nc.vector.quantize_mx(out=tq[:].bitcast(FP8X4), scales=ts[:], in_=st[:, lo : lo + GT * TILE_COLS])
             ready[g] = (tq, ts)
 
-        fill_src(0)
-        spread_dst(0)
-        transpose_edges(0)
-        move_edges(0)
-        for c in range(1, N_CHUNKS):
-            load_chunk(c)
-        fill_src(1)
-        fill_src(2)
-
         wsw = wsb[:].bitcast(F32).rearrange("p (r m e) -> p r m e", r=8, e=2)
         wg = const.tile([P, 4 * HID], BF16, name="wg", align_bytes=64)
         wgw = wg[:].bitcast(F32).rearrange("p (h e) -> p h e", e=2)
         wq = const.tile([P, HID], U32, name="wq", align_bytes=64)
         wsc = const.tile([P, HID], U8, name="wsc", align_bytes=64)
-        for rp in range(4):
-            wtp = mxp.tile([P, 512], F32, tag="mx")
-            for rl in range(2):
-                for e in range(2):
-                    col = (rl * 2 + e) * P
-                    nc.tensor.transpose(wtp[:, col : col + P], wsw[:, rp * 2 + rl, :, e], ident[:])
-            dst = wgw[:, rp * 256 : (rp + 1) * 256, :].rearrange("p (r q) e -> p r q e", r=2)
-            src = wtp[:].rearrange("p (r e q) -> p r q e", r=2, e=2)
-            if rp == 0:
-                nc.vector.tensor_copy(out=dst, in_=src)
-            else:
-                nc.scalar.copy(out=dst, in_=src)
-            if rp % 2 == 1:
-                hf = rp // 2
-                nc.vector.quantize_mx(
-                    out=wq[:, hf * HALF : (hf + 1) * HALF].bitcast(FP8X4),
-                    scales=wsc[:, hf * HALF : (hf + 1) * HALF],
-                    in_=wg[:, hf * 4 * HALF : (hf + 1) * 4 * HALF],
-                )
-            if rp == 1:
-                quantise(0)
+
+        def prepare_weights(hf):
+            for rp in range(2 * hf, 2 * hf + 2):
+                wtp = mxp.tile([P, 512], F32, tag="mx")
+                for rl in range(2):
+                    for e in range(2):
+                        col = (rl * 2 + e) * P
+                        nc.tensor.transpose(wtp[:, col : col + P], wsw[:, rp * 2 + rl, :, e], ident[:])
+                dst = wgw[:, rp * 256 : (rp + 1) * 256, :].rearrange("p (r q) e -> p r q e", r=2)
+                src = wtp[:].rearrange("p (r e q) -> p r q e", r=2, e=2)
+                if rp == 0:
+                    nc.vector.tensor_copy(out=dst, in_=src)
+                else:
+                    nc.scalar.copy(out=dst, in_=src)
+            nc.vector.quantize_mx(
+                out=wq[:, hf * HALF : (hf + 1) * HALF].bitcast(FP8X4),
+                scales=wsc[:, hf * HALF : (hf + 1) * HALF],
+                in_=wg[:, hf * 4 * HALF : (hf + 1) * 4 * HALF],
+            )
+
+        fill_src(0)
+        load_chunk(1)
+        spread_dst(0)
+        stage_first_group()
+        prepare_weights(0)
+        quantise(0)
+        transpose_edges(0)
+        move_edges(0)
+        load_chunk(2)
+        fill_src(1)
+        prepare_weights(1)
         spread_dst(1)
         transpose_edges(1)
-        move_edges(1)
+        for c in range(3, N_CHUNKS):
+            load_chunk(c)
+        fill_src(2)
 
         for g in range(N_GROUPS):
             c = g // 2
@@ -213,8 +243,8 @@ def tile_edge_update_only_pa_t_kernel(tc, node_fts, edge_fts, Wt, out):
                 nc.vector.tensor_tensor(out=o[:, col : col + HALF], in0=mx[:], in1=y[:], op=ALU.max)
                 if j == 1 and g + 1 < N_GROUPS:
                     quantise(g + 1)
-                if j == 1 and g % 2 == 1 and c + 2 < N_CHUNKS:
-                    move_edges(c + 2)
+                if j == 1 and (g == 0 or g % 2 == 1) and (g + 3) // 2 < N_CHUNKS:
+                    move_edges((g + 3) // 2)
                 if hf == 1 and (t + 1) % per_store == 0:
                     t0 = t + 1 - per_store
                     nc.sync.dma_start(

@@ -6,6 +6,7 @@ from concourse.masks import make_identity
 F32 = mybir.dt.float32
 BF16 = mybir.dt.bfloat16
 U32 = mybir.dt.uint32
+I32 = mybir.dt.int32
 U8 = mybir.dt.uint8
 FP8X4 = mybir.dt.float8_e4m3fn_x4
 ALU = mybir.AluOpType
@@ -22,10 +23,18 @@ N_GROUPS = N_NODE // GT
 CH = 8
 N_CHUNKS = N_NODE // CH
 N_SLOTS = 3
-PAD = 3
 NEG_SLOPE = 0.1
 TILE_COLS = 4 * P
 TILE_WORDS = EDGE_IN // 2
+CODE_B = 4 * P
+SCALE_B = P
+UNIT_B = CODE_B + SCALE_B
+UNIT_W = UNIT_B // 4
+CODE_W = CODE_B // 4
+SCALE_W = SCALE_B // 4
+DST_P = NODE_IN // 4
+DST_SCALE_P = 34
+REP = 4
 
 FLOPS = 2 * 2 * N_NODE * N_NODE * D_IN * HID
 
@@ -40,7 +49,6 @@ def tile_edge_update_only_pa_t_kernel(tc, node_fts, edge_fts, Wt, out):
     with ExitStack() as ctx:
         const = ctx.enter_context(tc.tile_pool(name="const", bufs=1))
         pkpool = ctx.enter_context(tc.tile_pool(name="pkpool", bufs=3))
-        qpool = ctx.enter_context(tc.tile_pool(name="qpool", bufs=3))
         ypool = ctx.enter_context(tc.tile_pool(name="ypool", bufs=4))
         opool = ctx.enter_context(tc.tile_pool(name="opool", bufs=4))
         tpp = ctx.enter_context(tc.psum_pool(name="tpp", bufs=2))
@@ -57,15 +65,12 @@ def tile_edge_update_only_pa_t_kernel(tc, node_fts, edge_fts, Wt, out):
 
         chunks = []
         for c in range(N_CHUNKS):
-            lead = PAD if c == 0 else 0
-            ec = const.tile([P, (lead + CH) * EDGE_IN], BF16, name="ec%d" % c)
+            ec = const.tile([P, CH * EDGE_IN], BF16, name="ec%d" % c)
             chunks.append(ec)
-        nc.vector.memset(chunks[0][:, 0 : PAD * EDGE_IN], 0.0)
 
         def load_chunk(c):
-            lead = PAD if c == 0 else 0
             nc.sync.dma_start(
-                out=chunks[c][:, lead * EDGE_IN :].rearrange("p (k f) -> p k f", f=EDGE_IN),
+                out=chunks[c][:].rearrange("p (k f) -> p k f", f=EDGE_IN),
                 in_=edge_v[:, c * CH : (c + 1) * CH, :],
             )
 
@@ -78,102 +83,125 @@ def tile_edge_update_only_pa_t_kernel(tc, node_fts, edge_fts, Wt, out):
             nc.sync.dma_start(out=wsb3[:, rows, NODE_IN : 2 * NODE_IN], in_=w_v[:, rows, 0:NODE_IN])
             nc.sync.dma_start(out=wsb3[:, rows, 2 * NODE_IN :], in_=w_v[:, rows, 2 * NODE_IN :])
 
-        ntp = tpp.tile([P, 512], F32, tag="tp")
+        npack = const.tile([P, UNIT_B], U8, name="npack", align_bytes=64)
+        n4c = const.tile([P, REP * P], U32, name="n4c", align_bytes=64)
+        n4s = const.tile([P, REP * P], U8, name="n4s", align_bytes=64)
+        nc.vector.memset(npack[:, CODE_B:UNIT_B].bitcast(I32), 0)
+        nc.vector.memset(n4s[:].bitcast(I32), 0)
+        packs = []
+        for s in range(N_SLOTS):
+            pt = const.tile([P, 2 * UNIT_B], U8, name="pack%d" % s, align_bytes=64)
+            nc.vector.memset(pt[:].bitcast(I32), 0)
+            packs.append(pt)
+        slots = []
+        for s in range(N_SLOTS):
+            st = const.tile([P, CH * UNIT_B], U8, name="st%d" % s, align_bytes=64)
+            slots.append(st)
+
         nrw = nr[:].bitcast(F32).rearrange("p (m e) -> p m e", e=2)
+        ntb = const.tile([P, TILE_COLS], BF16, name="ntb", align_bytes=64)
+        ntb4 = const.tile([P, REP * TILE_COLS], BF16, name="ntb4", align_bytes=64)
+        ntp = tpp.tile([P, 512], F32, tag="tp")
         for e in range(2):
             nc.tensor.transpose(ntp[:, e * P : (e + 1) * P], nrw[:, :, e], ident[:])
-        ntb = const.tile([P, TILE_COLS], BF16, name="ntb", align_bytes=64)
+        ntp4 = tpp.tile([P, 512], F32, tag="tp")
+        for e in range(2):
+            nc.tensor.transpose(ntp4[:, e * P : (e + 1) * P], nrw[:, :, e], ident[:])
         nc.vector.tensor_copy(
             out=ntb[:].bitcast(F32).rearrange("p (q e) -> p q e", e=2),
             in_=ntp[:, 0 : 2 * P].rearrange("p (e q) -> p q e", e=2),
         )
-
-        slots = []
-        for s in range(N_SLOTS):
-            st = const.tile([P, CH * TILE_COLS], BF16, name="st%d" % s, align_bytes=64)
-            slots.append(st)
+        nc.scalar.copy(
+            out=ntb4[:].bitcast(F32).rearrange("p (q r e) -> p q r e", r=REP, e=2),
+            in_=ntp4[:, 0 : 2 * P]
+            .rearrange("p (e q) -> p q e", e=2)
+            .unsqueeze(2)
+            .to_broadcast([P, P, REP, 2]),
+        )
+        nc.vector.quantize_mx(
+            out=npack[:, 0:CODE_B].bitcast(FP8X4), scales=npack[:, CODE_B:UNIT_B], in_=ntb[:]
+        )
+        nc.vector.quantize_mx(out=n4c[:].bitcast(FP8X4), scales=n4s[:], in_=ntb4[:])
 
         def fill_src(s):
             nc.sync.dma_start(
-                out=slots[s][48:96, :].rearrange("p (t c) -> p t c", t=CH),
-                in_=ntb[48:96, :].unsqueeze(1).to_broadcast([48, CH, TILE_COLS]),
+                out=slots[s][DST_P : 2 * DST_P, :].bitcast(I32).rearrange("p (t w) -> p t w", t=CH),
+                in_=npack[DST_P : 2 * DST_P, :].bitcast(I32).unsqueeze(1).to_broadcast([DST_P, CH, UNIT_W]),
+            )
+            nc.sync.dma_start(
+                out=slots[s][DST_SCALE_P:DST_P, :]
+                .bitcast(I32)
+                .rearrange("p (t w) -> p t w", t=CH)[:, :, CODE_W:UNIT_W],
+                in_=npack[DST_SCALE_P:DST_P, CODE_B:UNIT_B]
+                .bitcast(I32)
+                .unsqueeze(1)
+                .to_broadcast([DST_P - DST_SCALE_P, CH, SCALE_W]),
             )
 
-        def spread_dst(c):
-            st = slots[c % N_SLOTS]
-            for gl in range(2):
-                for b in range(2):
-                    k0 = c * CH + gl * GT
-                    nc.gpsimd.tensor_scalar(
-                        out=st[0:48, gl * GT * TILE_COLS : (gl + 1) * GT * TILE_COLS].rearrange(
-                            "p (t b i j) -> p t b i j", t=GT, b=2, j=4
-                        )[:, :, b, :, :],
-                        in0=ntb[0:48, :]
-                        .rearrange("p (b k j) -> p b k j", b=2, j=4)[:, b, k0 : k0 + GT, :]
-                        .unsqueeze(2)
-                        .to_broadcast([48, GT, N_NODE, 4]),
-                        scalar1=1.0,
-                        scalar2=0.0,
-                        op0=ALU.mult,
-                        op1=ALU.add,
-                    )
-
-        def transpose_window(bank, slot, words):
-            win = words.rearrange("p (m e) -> p m e", e=2)
-            for e in range(2):
-                col = (2 * slot + e) * P
-                nc.tensor.transpose(bank[:, col : col + P], win[:, :, e], ident[:])
-
-        def stage_first_group():
-            padded = chunks[0][:].bitcast(F32)
-            stw = slots[0][:].bitcast(F32).rearrange("p (t q e) -> p t q e", t=CH, e=2)
-            for pair in range(GT // 2):
-                bank = tpp.tile([P, 512], F32, tag="tp")
-                for tl in range(2):
-                    t = 2 * pair + tl
-                    transpose_window(bank, tl, padded[:, t * TILE_WORDS : (t + GT) * TILE_WORDS])
-                nc.scalar.copy(
-                    out=stw[96:128, 2 * pair : 2 * pair + 2, :, :],
-                    in_=bank[96:128, :].rearrange("p (t e q) -> p t q e", t=2, e=2),
+        def spread_dst(g):
+            st = slots[(g // 2) % N_SLOTS]
+            t0 = (g % 2) * GT
+            codes = npack[0:DST_P, 0:CODE_B].bitcast(U32).rearrange("p (b k) -> p b k", b=2)
+            for tl in range(GT):
+                k = g * GT + tl
+                lo = (t0 + tl) * UNIT_B
+                nc.gpsimd.tensor_copy(
+                    out=st[0:DST_P, lo : lo + CODE_B].bitcast(U32).rearrange("p (b i) -> p b i", b=2),
+                    in_=codes[:, :, k : k + 1].to_broadcast([DST_P, 2, N_NODE]),
                 )
-
-        def chunk_groups(c):
-            return range(1, 2) if c == 0 else range(2)
+            nc.gpsimd.tensor_copy(
+                out=st[0:DST_SCALE_P, t0 * UNIT_B : (t0 + GT) * UNIT_B]
+                .bitcast(U32)
+                .rearrange("p (t w) -> p t w", t=GT)[:, :, CODE_W:UNIT_W]
+                .rearrange("p t (b i) -> p t b i", b=2),
+                in_=n4s[0:DST_SCALE_P, :]
+                .bitcast(U32)
+                .rearrange("p (b k) -> p k b", b=2)[:, g * GT : (g + 1) * GT, :]
+                .unsqueeze(3)
+                .to_broadcast([DST_SCALE_P, GT, 2, SCALE_W // 2]),
+            )
 
         banks = {}
+        staged = {}
 
         def transpose_edges(c):
-            lead = PAD if c == 0 else 0
             words = chunks[c][:].bitcast(F32)
             bank = tpp.tile([P, 512], F32, tag="tp")
-            for gl in chunk_groups(c):
-                w0 = (lead + gl * GT) * TILE_WORDS
-                transpose_window(bank, gl, words[:, w0 : w0 + GT * TILE_WORDS])
+            for gl in range(2):
+                win = words[:, gl * GT * TILE_WORDS : (gl + 1) * GT * TILE_WORDS].rearrange(
+                    "p (m e) -> p m e", e=2
+                )
+                for e in range(2):
+                    col = (2 * gl + e) * P
+                    nc.tensor.transpose(bank[:, col : col + P], win[:, :, e], ident[:])
             banks[c] = bank
+
+        def evacuate_edges(c):
+            pk = pkpool.tile([P, 2 * TILE_COLS], BF16, tag="pk", align_bytes=64)
+            nc.scalar.copy(
+                out=pk[:].bitcast(F32).rearrange("p (g q e) -> p g q e", g=2, e=2),
+                in_=banks[c][:].rearrange("p (g e q) -> p g q e", g=2, e=2),
+            )
+            staged[c] = pk
+
+        def quantise_edges(c):
+            pack = packs[c % N_SLOTS]
+            for gl in range(2):
+                lo = gl * UNIT_B
+                nc.vector.quantize_mx(
+                    out=pack[:, lo : lo + CODE_B].bitcast(FP8X4),
+                    scales=pack[:, lo + CODE_B : lo + UNIT_B],
+                    in_=staged[c][:, gl * TILE_COLS : (gl + 1) * TILE_COLS],
+                )
 
         def move_edges(c):
             st = slots[c % N_SLOTS]
-            groups = slice(chunk_groups(c)[0], 2)
-            pk = pkpool.tile([P, 2 * TILE_COLS], BF16, tag="pk")
-            nc.scalar.copy(
-                out=pk[:].bitcast(F32).rearrange("p (g q e) -> p g q e", g=2, e=2)[:, groups, :, :],
-                in_=banks[c][:].rearrange("p (g e q) -> p g q e", g=2, e=2)[:, groups, :, :],
-            )
-            for n in range(4):
+            pack = packs[c % N_SLOTS]
+            for n in range(GT):
                 nc.sync.dma_start(
-                    out=st[96:128, :].rearrange("p (g n c) -> p g n c", g=2, n=4)[:, groups, n, :],
-                    in_=pk[32 * n : 32 * n + 32, :].rearrange("p (g c) -> p g c", g=2)[:, groups, :],
+                    out=st[96:128, :].bitcast(I32).rearrange("p (g n w) -> p g n w", g=2, n=GT)[:, :, n, :],
+                    in_=pack[32 * n : 32 * n + 32, :].bitcast(I32).rearrange("p (g w) -> p g w", g=2),
                 )
-
-        ready = {}
-
-        def quantise(g):
-            st = slots[(g // 2) % N_SLOTS]
-            tq = qpool.tile([P, GT * P], U32, tag="tq", align_bytes=64)
-            ts = qpool.tile([P, GT * P], U8, tag="ts", align_bytes=64)
-            lo = (g % 2) * GT * TILE_COLS
-            nc.vector.quantize_mx(out=tq[:].bitcast(FP8X4), scales=ts[:], in_=st[:, lo : lo + GT * TILE_COLS])
-            ready[g] = (tq, ts)
 
         wsw = wsb[:].bitcast(F32).rearrange("p (r m e) -> p r m e", r=8, e=2)
         wg = const.tile([P, 4 * HID], BF16, name="wg", align_bytes=64)
@@ -200,18 +228,20 @@ def tile_edge_update_only_pa_t_kernel(tc, node_fts, edge_fts, Wt, out):
                 in_=wg[:, hf * 4 * HALF : (hf + 1) * 4 * HALF],
             )
 
-        fill_src(0)
         load_chunk(1)
+        fill_src(0)
         spread_dst(0)
-        stage_first_group()
-        prepare_weights(0)
-        quantise(0)
+        spread_dst(1)
         transpose_edges(0)
+        evacuate_edges(0)
+        quantise_edges(0)
         move_edges(0)
         load_chunk(2)
         fill_src(1)
+        prepare_weights(0)
         prepare_weights(1)
-        spread_dst(1)
+        spread_dst(2)
+        spread_dst(3)
         transpose_edges(1)
         for c in range(3, N_CHUNKS):
             load_chunk(c)
@@ -219,19 +249,22 @@ def tile_edge_update_only_pa_t_kernel(tc, node_fts, edge_fts, Wt, out):
 
         for g in range(N_GROUPS):
             c = g // 2
-            tq, ts = ready[g]
+            st = slots[c % N_SLOTS]
             o = opool.tile([P, GT * HID], F32, tag="o")
             per_store = 1 if g == 0 or g >= N_GROUPS - 2 else 2
+            nxt = (g + 3) // 2 if (g == 0 or g % 2 == 1) and (g + 3) // 2 < N_CHUNKS else None
             if g % 2 == 0 and c + 2 < N_CHUNKS:
-                spread_dst(c + 2)
+                spread_dst(2 * (c + 2))
+                spread_dst(2 * (c + 2) + 1)
             for j in range(2 * GT):
                 t = j // 2
                 hf = j % 2
+                lo = ((g % 2) * GT + t) * UNIT_B
                 mx = mxp.tile([P, HALF], F32, tag="mx")
                 nc.tensor.matmul_mx(
                     out=mx[:],
-                    lhsT=tq[:, t * P : (t + 1) * P].bitcast(FP8X4),
-                    lhsT_scale=ts[:, t * P : (t + 1) * P],
+                    lhsT=st[:, lo : lo + CODE_B].bitcast(FP8X4),
+                    lhsT_scale=st[:, lo + CODE_B : lo + UNIT_B],
                     rhs=wq[:, hf * HALF : (hf + 1) * HALF].bitcast(FP8X4),
                     rhs_scale=wsc[:, hf * HALF : (hf + 1) * HALF],
                     start=True,
@@ -241,15 +274,16 @@ def tile_edge_update_only_pa_t_kernel(tc, node_fts, edge_fts, Wt, out):
                 nc.scalar.mul(out=y[:], in_=mx[:], mul=NEG_SLOPE)
                 col = t * HID + hf * HALF
                 nc.vector.tensor_tensor(out=o[:, col : col + HALF], in0=mx[:], in1=y[:], op=ALU.max)
-                if j == 1 and g + 1 < N_GROUPS:
-                    quantise(g + 1)
-                if j == 1 and (g == 0 or g % 2 == 1) and (g + 3) // 2 < N_CHUNKS:
-                    move_edges((g + 3) // 2)
+                if j == 1 and nxt is not None:
+                    evacuate_edges(nxt)
                 if hf == 1 and (t + 1) % per_store == 0:
                     t0 = t + 1 - per_store
                     nc.sync.dma_start(
                         out=out_v[:, g * GT + t0 : g * GT + t + 1, :],
                         in_=o[:, t0 * HID : (t + 1) * HID].rearrange("p (t h) -> p t h", t=per_store),
                     )
+                if j == 3 and nxt is not None:
+                    quantise_edges(nxt)
+                    move_edges(nxt)
             if g % 2 == 0 and c + 2 < N_CHUNKS:
                 transpose_edges(c + 2)

@@ -10,6 +10,7 @@ I32 = mybir.dt.int32
 U8 = mybir.dt.uint8
 FP8X4 = mybir.dt.float8_e4m3fn_x4
 ALU = mybir.AluOpType
+ACT = mybir.ActivationFunctionType
 
 P = 128
 N_NODE = 64
@@ -271,7 +272,7 @@ def tile_edge_update_only_pa_t_kernel(tc, node_fts, edge_fts, Wt, out):
                     stop=True,
                 )
                 y = ypool.tile([P, HALF], F32, tag="y")
-                nc.scalar.mul(out=y[:], in_=mx[:], mul=NEG_SLOPE)
+                nc.scalar.activation(out=y[:], in_=mx[:], func=ACT.Copy, scale=NEG_SLOPE)
                 col = t * HID + hf * HALF
                 nc.vector.tensor_tensor(out=o[:, col : col + HALF], in0=mx[:], in1=y[:], op=ALU.max)
                 if j == 1 and nxt is not None:

@@ -36,6 +36,7 @@ SCALE_W = SCALE_B // 4
 DST_P = NODE_IN // 4
 DST_SCALE_P = 34
 REP = 4
+FLT_MAX = 3.4028234663852886e38
 
 FLOPS = 2 * 2 * N_NODE * N_NODE * D_IN * HID
 
@@ -52,6 +53,7 @@ def tile_edge_update_only_pa_t_kernel(tc, node_fts, edge_fts, Wt, out):
         pkpool = ctx.enter_context(tc.tile_pool(name="pkpool", bufs=3))
         ypool = ctx.enter_context(tc.tile_pool(name="ypool", bufs=4))
         opool = ctx.enter_context(tc.tile_pool(name="opool", bufs=4))
+        xpool = ctx.enter_context(tc.tile_pool(name="xpool", bufs=2))
         tpp = ctx.enter_context(tc.psum_pool(name="tpp", bufs=2))
         mxp = ctx.enter_context(tc.psum_pool(name="mxp", bufs=6))
         ctx.enter_context(tc.manual_schedule())
@@ -248,18 +250,21 @@ def tile_edge_update_only_pa_t_kernel(tc, node_fts, edge_fts, Wt, out):
             load_chunk(c)
         fill_src(2)
 
+        natural = [(t, hf) for t in range(GT) for hf in range(2)]
         for g in range(N_GROUPS):
             c = g // 2
             st = slots[c % N_SLOTS]
             o = opool.tile([P, GT * HID], F32, tag="o")
-            per_store = 1 if g == 0 or g >= N_GROUPS - 2 else 2
             nxt = (g + 3) // 2 if (g == 0 or g % 2 == 1) and (g + 3) // 2 < N_CHUNKS else None
-            if g % 2 == 0 and c + 2 < N_CHUNKS:
+            offload = g % 2 == 0 and g >= 2
+            per_store = 1 if g == 0 or g >= N_GROUPS - 2 else 2
+            order = [natural[-1]] + natural[:-1] if offload else natural
+            if g == 0:
                 spread_dst(2 * (c + 2))
                 spread_dst(2 * (c + 2) + 1)
+            seen = set()
             for j in range(2 * GT):
-                t = j // 2
-                hf = j % 2
+                t, hf = order[j]
                 lo = ((g % 2) * GT + t) * UNIT_B
                 mx = mxp.tile([P, HALF], F32, tag="mx")
                 nc.tensor.matmul_mx(
@@ -271,19 +276,33 @@ def tile_edge_update_only_pa_t_kernel(tc, node_fts, edge_fts, Wt, out):
                     start=True,
                     stop=True,
                 )
-                y = ypool.tile([P, HALF], F32, tag="y")
-                nc.scalar.activation(out=y[:], in_=mx[:], func=ACT.Copy, scale=NEG_SLOPE)
                 col = t * HID + hf * HALF
-                nc.vector.tensor_tensor(out=o[:, col : col + HALF], in0=mx[:], in1=y[:], op=ALU.max)
+                res = o[:, col : col + HALF]
+                if offload and j == 0:
+                    nc.scalar.copy(out=res, in_=mx[:])
+                    x = xpool.tile([P, HALF], F32, tag="x")
+                    nc.gpsimd.tensor_scalar(
+                        out=x[:], in0=res, scalar1=NEG_SLOPE - 1.0, scalar2=0.0, op0=ALU.mult, op1=ALU.add
+                    )
+                    nc.gpsimd.tensor_scalar(out=x[:], in0=x[:], scalar1=FLT_MAX, scalar2=0.0, op0=ALU.min, op1=ALU.max)
+                    nc.gpsimd.tensor_tensor(out=res, in0=res, in1=x[:], op=ALU.add)
+                    if c + 2 < N_CHUNKS:
+                        spread_dst(2 * (c + 2))
+                        spread_dst(2 * (c + 2) + 1)
+                else:
+                    y = ypool.tile([P, HALF], F32, tag="y")
+                    nc.scalar.activation(out=y[:], in_=mx[:], func=ACT.Copy, scale=NEG_SLOPE)
+                    nc.vector.tensor_tensor(out=res, in0=mx[:], in1=y[:], op=ALU.max)
+                seen.add((t, hf))
                 if j == 1 and nxt is not None:
                     evacuate_edges(nxt)
-                if hf == 1 and (t + 1) % per_store == 0:
-                    t0 = t + 1 - per_store
+                t0 = t - t % per_store
+                if all((tt, hh) in seen for tt in range(t0, t0 + per_store) for hh in range(2)):
                     nc.sync.dma_start(
-                        out=out_v[:, g * GT + t0 : g * GT + t + 1, :],
-                        in_=o[:, t0 * HID : (t + 1) * HID].rearrange("p (t h) -> p t h", t=per_store),
+                        out=out_v[:, g * GT + t0 : g * GT + t0 + per_store, :],
+                        in_=o[:, t0 * HID : (t0 + per_store) * HID].rearrange("p (t h) -> p t h", t=per_store),
                     )
-                if j == 3 and nxt is not None:
+                if j == (3 if g == 0 else 7) and nxt is not None:
                     quantise_edges(nxt)
                     move_edges(nxt)
             if g % 2 == 0 and c + 2 < N_CHUNKS:

@@ -36,6 +36,7 @@ SCALE_W = SCALE_B // 4
 DST_P = NODE_IN // 4
 DST_SCALE_P = 34
 REP = 4
+ON_VECTOR = (3, 5, 7)
 FLT_MAX = 3.4028234663852886e38
 
 FLOPS = 2 * 2 * N_NODE * N_NODE * D_IN * HID
@@ -181,7 +182,8 @@ def tile_edge_update_only_pa_t_kernel(tc, node_fts, edge_fts, Wt, out):
 
         def evacuate_edges(c):
             pk = pkpool.tile([P, 2 * TILE_COLS], BF16, tag="pk", align_bytes=64)
-            nc.scalar.copy(
+            copier = nc.vector.tensor_copy if c in ON_VECTOR else nc.scalar.copy
+            copier(
                 out=pk[:].bitcast(F32).rearrange("p (g q e) -> p g q e", g=2, e=2),
                 in_=banks[c][:].rearrange("p (g e q) -> p g q e", g=2, e=2),
             )

@@ -36,6 +36,7 @@ SCALE_W = SCALE_B // 4
 DST_P = NODE_IN // 4
 DST_SCALE_P = 34
 REP = 4
+Y_BUFS = 4
 ON_VECTOR = (3, 5, 7)
 FLT_MAX = 3.4028234663852886e38
 
@@ -52,7 +53,7 @@ def tile_edge_update_only_pa_t_kernel(tc, node_fts, edge_fts, Wt, out):
     with ExitStack() as ctx:
         const = ctx.enter_context(tc.tile_pool(name="const", bufs=1))
         pkpool = ctx.enter_context(tc.tile_pool(name="pkpool", bufs=3))
-        ypool = ctx.enter_context(tc.tile_pool(name="ypool", bufs=4))
+        ypool = ctx.enter_context(tc.tile_pool(name="ypool", bufs=Y_BUFS))
         opool = ctx.enter_context(tc.tile_pool(name="opool", bufs=4))
         xpool = ctx.enter_context(tc.tile_pool(name="xpool", bufs=2))
         tpp = ctx.enter_context(tc.psum_pool(name="tpp", bufs=2))
@@ -253,6 +254,16 @@ def tile_edge_update_only_pa_t_kernel(tc, node_fts, edge_fts, Wt, out):
         fill_src(2)
 
         natural = [(t, hf) for t in range(GT) for hf in range(2)]
+        deferred = []
+        issued = 0
+        banks_done = 0
+
+        def store(queue, o, g, t0, n):
+            queue.dma_start(
+                out=out_v[:, g * GT + t0 : g * GT + t0 + n, :],
+                in_=o[:, t0 * HID : (t0 + n) * HID].rearrange("p (t h) -> p t h", t=n),
+            )
+
         for g in range(N_GROUPS):
             c = g // 2
             st = slots[c % N_SLOTS]
@@ -298,12 +309,16 @@ def tile_edge_update_only_pa_t_kernel(tc, node_fts, edge_fts, Wt, out):
                 seen.add((t, hf))
                 if j == 1 and nxt is not None:
                     evacuate_edges(nxt)
+                banks_done += 1
+                if issued < len(deferred) and deferred[issued][0] <= banks_done:
+                    store(nc.scalar, *deferred[issued][1:])
+                    issued += 1
                 t0 = t - t % per_store
                 if all((tt, hh) in seen for tt in range(t0, t0 + per_store) for hh in range(2)):
-                    nc.sync.dma_start(
-                        out=out_v[:, g * GT + t0 : g * GT + t0 + per_store, :],
-                        in_=o[:, t0 * HID : (t0 + per_store) * HID].rearrange("p (t h) -> p t h", t=per_store),
-                    )
+                    if per_store == 2 and t0 == 2:
+                        deferred.append((banks_done + Y_BUFS + 1, o, g, t0, per_store))
+                    else:
+                        store(nc.sync, o, g, t0, per_store)
                 if j == (3 if g == 0 else 7) and nxt is not None:
                     quantise_edges(nxt)
                     move_edges(nxt)

@@ -36,7 +36,7 @@ SCALE_W = SCALE_B // 4
 DST_P = NODE_IN // 4
 DST_SCALE_P = 34
 REP = 4
-Y_BUFS = 4
+Y_BUFS = 8
 ON_VECTOR = (3, 5, 7)
 FLT_MAX = 3.4028234663852886e38
 
@@ -254,12 +254,9 @@ def tile_edge_update_only_pa_t_kernel(tc, node_fts, edge_fts, Wt, out):
         fill_src(2)
 
         natural = [(t, hf) for t in range(GT) for hf in range(2)]
-        deferred = []
-        issued = 0
-        banks_done = 0
 
-        def store(queue, o, g, t0, n):
-            queue.dma_start(
+        def store(o, g, t0, n):
+            nc.sync.dma_start(
                 out=out_v[:, g * GT + t0 : g * GT + t0 + n, :],
                 in_=o[:, t0 * HID : (t0 + n) * HID].rearrange("p (t h) -> p t h", t=n),
             )
@@ -309,16 +306,9 @@ def tile_edge_update_only_pa_t_kernel(tc, node_fts, edge_fts, Wt, out):
                 seen.add((t, hf))
                 if j == 1 and nxt is not None:
                     evacuate_edges(nxt)
-                banks_done += 1
-                if issued < len(deferred) and deferred[issued][0] <= banks_done:
-                    store(nc.scalar, *deferred[issued][1:])
-                    issued += 1
                 t0 = t - t % per_store
                 if all((tt, hh) in seen for tt in range(t0, t0 + per_store) for hh in range(2)):
-                    if per_store == 2 and t0 == 2:
-                        deferred.append((banks_done + Y_BUFS + 1, o, g, t0, per_store))
-                    else:
-                        store(nc.sync, o, g, t0, per_store)
+                    store(o, g, t0, per_store)
                 if j == (3 if g == 0 else 7) and nxt is not None:
                     quantise_edges(nxt)
                     move_edges(nxt)

@@ -19,6 +19,7 @@ EDGE_IN = 128
 D_IN = 512
 HID = 1024
 HALF = 512
+QUARTER = 256
 GT = 4
 N_GROUPS = N_NODE // GT
 CH = 8
@@ -36,8 +37,8 @@ SCALE_W = SCALE_B // 4
 DST_P = NODE_IN // 4
 DST_SCALE_P = 34
 REP = 4
+LAST = GT - 1
 Y_BUFS = 8
-ON_VECTOR = (3, 5, 7)
 FLT_MAX = 3.4028234663852886e38
 
 FLOPS = 2 * 2 * N_NODE * N_NODE * D_IN * HID
@@ -61,116 +62,121 @@ def tile_edge_update_only_pa_t_kernel(tc, node_fts, edge_fts, Wt, out):
         ctx.enter_context(tc.manual_schedule())
 
         ident = const.tile([P, P], F32, name="ident")
-        make_identity(nc, ident[:])
-
         nr = const.tile([P, D_IN], BF16, name="nr")
-        nc.sync.dma_start(out=nr[:, 0:NODE_IN], in_=node_rows)
-        nc.sync.dma_start(out=nr[:, NODE_IN : 2 * NODE_IN], in_=node_rows)
-        nc.vector.memset(nr[:, 2 * NODE_IN : D_IN], 0.0)
-
-        chunks = []
-        for c in range(N_CHUNKS):
-            ec = const.tile([P, CH * EDGE_IN], BF16, name="ec%d" % c)
-            chunks.append(ec)
-
-        def load_chunk(c):
-            nc.sync.dma_start(
-                out=chunks[c][:].rearrange("p (k f) -> p k f", f=EDGE_IN),
-                in_=edge_v[:, c * CH : (c + 1) * CH, :],
-            )
-
-        load_chunk(0)
+        edges = []
+        for c, n in ((0, 1), (1, 1), (2, 2), (4, 2), (6, 2)):
+            ec = const.tile([P, n * CH * EDGE_IN], BF16, name="ec%d" % c)
+            edges.append((c, n, ec))
         wsb = const.tile([P, 8 * D_IN], BF16, name="wsb")
-        wsb3 = wsb[:].rearrange("p (r k) -> p r k", r=8)
-        for hf in range(2):
-            rows = slice(hf * 4, hf * 4 + 4)
-            nc.sync.dma_start(out=wsb3[:, rows, 0:NODE_IN], in_=w_v[:, rows, NODE_IN : 2 * NODE_IN])
-            nc.sync.dma_start(out=wsb3[:, rows, NODE_IN : 2 * NODE_IN], in_=w_v[:, rows, 0:NODE_IN])
-            nc.sync.dma_start(out=wsb3[:, rows, 2 * NODE_IN :], in_=w_v[:, rows, 2 * NODE_IN :])
-
         npack = const.tile([P, UNIT_B], U8, name="npack", align_bytes=64)
         n4c = const.tile([P, REP * P], U32, name="n4c", align_bytes=64)
         n4s = const.tile([P, REP * P], U8, name="n4s", align_bytes=64)
-        nc.vector.memset(npack[:, CODE_B:UNIT_B].bitcast(I32), 0)
-        nc.vector.memset(n4s[:].bitcast(I32), 0)
+        ntb = const.tile([P, TILE_COLS], BF16, name="ntb", align_bytes=64)
+        ntb4 = const.tile([P, REP * TILE_COLS], BF16, name="ntb4", align_bytes=64)
         packs = []
         for s in range(N_SLOTS):
             pt = const.tile([P, 2 * UNIT_B], U8, name="pack%d" % s, align_bytes=64)
-            nc.vector.memset(pt[:].bitcast(I32), 0)
             packs.append(pt)
         slots = []
         for s in range(N_SLOTS):
             st = const.tile([P, CH * UNIT_B], U8, name="st%d" % s, align_bytes=64)
             slots.append(st)
+        lead = const.tile([P, 2 * UNIT_B], U8, name="lead", align_bytes=64)
+        wg = const.tile([P, 4 * HID], BF16, name="wg", align_bytes=64)
+        wq = const.tile([P, HID], U32, name="wq", align_bytes=64)
+        wsc = const.tile([P, HID], U8, name="wsc", align_bytes=64)
+        o8 = const.tile([P, CH * HID], F32, name="o8")
 
-        nrw = nr[:].bitcast(F32).rearrange("p (m e) -> p m e", e=2)
-        ntb = const.tile([P, TILE_COLS], BF16, name="ntb", align_bytes=64)
-        ntb4 = const.tile([P, REP * TILE_COLS], BF16, name="ntb4", align_bytes=64)
-        ntp = tpp.tile([P, 512], F32, tag="tp")
-        for e in range(2):
-            nc.tensor.transpose(ntp[:, e * P : (e + 1) * P], nrw[:, :, e], ident[:])
-        ntp4 = tpp.tile([P, 512], F32, tag="tp")
-        for e in range(2):
-            nc.tensor.transpose(ntp4[:, e * P : (e + 1) * P], nrw[:, :, e], ident[:])
-        nc.vector.tensor_copy(
-            out=ntb[:].bitcast(F32).rearrange("p (q e) -> p q e", e=2),
-            in_=ntp[:, 0 : 2 * P].rearrange("p (e q) -> p q e", e=2),
-        )
-        nc.scalar.copy(
-            out=ntb4[:].bitcast(F32).rearrange("p (q r e) -> p q r e", r=REP, e=2),
-            in_=ntp4[:, 0 : 2 * P]
-            .rearrange("p (e q) -> p q e", e=2)
-            .unsqueeze(2)
-            .to_broadcast([P, P, REP, 2]),
-        )
-        nc.vector.quantize_mx(
-            out=npack[:, 0:CODE_B].bitcast(FP8X4), scales=npack[:, CODE_B:UNIT_B], in_=ntb[:]
-        )
-        nc.vector.quantize_mx(out=n4c[:].bitcast(FP8X4), scales=n4s[:], in_=ntb4[:])
+        wsb3 = wsb[:].rearrange("p (r k) -> p r k", r=8)
 
-        def fill_src(s):
+        def load_weights(r0, n):
+            rows = slice(r0, r0 + n)
+            nc.sync.dma_start(out=wsb3[:, rows, 0:NODE_IN], in_=w_v[:, rows, NODE_IN : 2 * NODE_IN])
+            nc.sync.dma_start(out=wsb3[:, rows, NODE_IN : 2 * NODE_IN], in_=w_v[:, rows, 0:NODE_IN])
+            nc.sync.dma_start(out=wsb3[:, rows, 2 * NODE_IN :], in_=w_v[:, rows, 2 * NODE_IN :])
+
+        def load_edges(x):
+            c, n, ec = edges[x]
             nc.sync.dma_start(
-                out=slots[s][DST_P : 2 * DST_P, :].bitcast(I32).rearrange("p (t w) -> p t w", t=CH),
-                in_=npack[DST_P : 2 * DST_P, :].bitcast(I32).unsqueeze(1).to_broadcast([DST_P, CH, UNIT_W]),
-            )
-            nc.sync.dma_start(
-                out=slots[s][DST_SCALE_P:DST_P, :]
-                .bitcast(I32)
-                .rearrange("p (t w) -> p t w", t=CH)[:, :, CODE_W:UNIT_W],
-                in_=npack[DST_SCALE_P:DST_P, CODE_B:UNIT_B]
-                .bitcast(I32)
-                .unsqueeze(1)
-                .to_broadcast([DST_P - DST_SCALE_P, CH, SCALE_W]),
+                out=ec[:].rearrange("p (k f) -> p k f", f=EDGE_IN),
+                in_=edge_v[:, c * CH : (c + n) * CH, :],
             )
 
-        def spread_dst(g):
+        nc.sync.dma_start(
+            out=nr[:, 0 : 2 * NODE_IN].rearrange("p (s f) -> p s f", s=2),
+            in_=node_rows.unsqueeze(1).to_broadcast([P, 2, NODE_IN]),
+        )
+        load_edges(0)
+        load_weights(0, 2)
+        load_weights(2, 2)
+        load_weights(4, 4)
+        load_edges(1)
+
+        make_identity(nc, ident[:])
+        nc.vector.memset(nr[:, 2 * NODE_IN : D_IN], 0.0)
+        nc.vector.memset(npack[:, CODE_B:UNIT_B].bitcast(I32), 0)
+        nc.vector.memset(n4s[:].bitcast(I32), 0)
+        nc.vector.memset(slots[0][:].bitcast(I32), 0)
+        for pt in packs:
+            nc.vector.memset(pt[:].bitcast(I32), 0)
+
+        def fill_lead():
+            for p0 in (32, 64):
+                nc.vector.tensor_copy(
+                    out=lead[p0 : p0 + 32, :].bitcast(I32).rearrange("p (t w) -> p t w", t=2),
+                    in_=npack[p0 : p0 + 32, :].bitcast(I32).unsqueeze(1).to_broadcast([32, 2, UNIT_W]),
+                )
+
+        def fill_rows(s, p0, n, lo, hi):
+            nc.sync.dma_start(
+                out=slots[s][p0 : p0 + n, :].bitcast(I32).rearrange("p (t w) -> p t w", t=CH)[:, :, lo:hi],
+                in_=npack[p0 : p0 + n, 4 * lo : 4 * hi].bitcast(I32).unsqueeze(1).to_broadcast([n, CH, hi - lo]),
+            )
+
+        def fill_slot(s):
+            for p0 in (32, 64):
+                nc.gpsimd.tensor_copy(
+                    out=slots[s][p0 : p0 + 32, :].bitcast(U32).rearrange("p (t w) -> p t w", t=CH),
+                    in_=npack[p0 : p0 + 32, :].bitcast(U32).unsqueeze(1).to_broadcast([32, CH, UNIT_W]),
+                )
+
+        def spread_codes(dst, t0, nt, src):
+            nc.gpsimd.tensor_copy(
+                out=dst[0:DST_P, t0 * UNIT_B : (t0 + nt) * UNIT_B]
+                .bitcast(U32)
+                .rearrange("p (t w) -> p t w", t=nt)[:, :, 0:CODE_W]
+                .rearrange("p t (b i) -> p t b i", b=2),
+                in_=src.unsqueeze(3).to_broadcast([DST_P, nt, 2, N_NODE]),
+            )
+
+        def spread_scales(dst, t0, nt, src):
+            nc.gpsimd.tensor_copy(
+                out=dst[0:DST_SCALE_P, t0 * UNIT_B : (t0 + nt) * UNIT_B]
+                .bitcast(U32)
+                .rearrange("p (t w) -> p t w", t=nt)[:, :, CODE_W:UNIT_W]
+                .rearrange("p t (b i) -> p t b i", b=2),
+                in_=src.unsqueeze(3).to_broadcast([DST_SCALE_P, nt, 2, SCALE_W // 2]),
+            )
+
+        codes_k = npack[0:DST_P, 0:CODE_B].bitcast(U32).rearrange("p (b k) -> p k b", b=2)
+        scales_k = n4s[0:DST_SCALE_P, :].bitcast(U32).rearrange("p (b k) -> p k b", b=2)
+        codes_n = npack[0:DST_P, 0:CODE_B].bitcast(U32).rearrange("p (b g n) -> p n g b", b=2, n=GT)
+        scales_n = n4s[0:DST_SCALE_P, :].bitcast(U32).rearrange("p (b g n) -> p n g b", b=2, n=GT)
+
+        def spread_group(g, codes=True, scales=True):
             st = slots[(g // 2) % N_SLOTS]
             t0 = (g % 2) * GT
-            codes = npack[0:DST_P, 0:CODE_B].bitcast(U32).rearrange("p (b k) -> p b k", b=2)
-            for tl in range(GT):
-                k = g * GT + tl
-                lo = (t0 + tl) * UNIT_B
-                nc.gpsimd.tensor_copy(
-                    out=st[0:DST_P, lo : lo + CODE_B].bitcast(U32).rearrange("p (b i) -> p b i", b=2),
-                    in_=codes[:, :, k : k + 1].to_broadcast([DST_P, 2, N_NODE]),
-                )
-            nc.gpsimd.tensor_copy(
-                out=st[0:DST_SCALE_P, t0 * UNIT_B : (t0 + GT) * UNIT_B]
-                .bitcast(U32)
-                .rearrange("p (t w) -> p t w", t=GT)[:, :, CODE_W:UNIT_W]
-                .rearrange("p t (b i) -> p t b i", b=2),
-                in_=n4s[0:DST_SCALE_P, :]
-                .bitcast(U32)
-                .rearrange("p (b k) -> p k b", b=2)[:, g * GT : (g + 1) * GT, :]
-                .unsqueeze(3)
-                .to_broadcast([DST_SCALE_P, GT, 2, SCALE_W // 2]),
-            )
+            if codes:
+                spread_codes(st, t0, GT, codes_k[:, g * GT : (g + 1) * GT, :])
+            if scales:
+                spread_scales(st, t0, GT, scales_k[:, g * GT : (g + 1) * GT, :])
 
         banks = {}
         staged = {}
 
         def transpose_edges(c):
-            words = chunks[c][:].bitcast(F32)
+            c0, tile_bf = [(e0, et) for e0, en, et in edges if e0 <= c < e0 + en][0]
+            words = tile_bf[:, (c - c0) * CH * EDGE_IN : (c - c0 + 1) * CH * EDGE_IN].bitcast(F32)
             bank = tpp.tile([P, 512], F32, tag="tp")
             for gl in range(2):
                 win = words[:, gl * GT * TILE_WORDS : (gl + 1) * GT * TILE_WORDS].rearrange(
@@ -181,9 +187,8 @@ def tile_edge_update_only_pa_t_kernel(tc, node_fts, edge_fts, Wt, out):
                     nc.tensor.transpose(bank[:, col : col + P], win[:, :, e], ident[:])
             banks[c] = bank
 
-        def evacuate_edges(c):
+        def evacuate_edges(copier, c):
             pk = pkpool.tile([P, 2 * TILE_COLS], BF16, tag="pk", align_bytes=64)
-            copier = nc.vector.tensor_copy if c in ON_VECTOR else nc.scalar.copy
             copier(
                 out=pk[:].bitcast(F32).rearrange("p (g q e) -> p g q e", g=2, e=2),
                 in_=banks[c][:].rearrange("p (g e q) -> p g q e", g=2, e=2),
@@ -203,89 +208,187 @@ def tile_edge_update_only_pa_t_kernel(tc, node_fts, edge_fts, Wt, out):
         def move_edges(c):
             st = slots[c % N_SLOTS]
             pack = packs[c % N_SLOTS]
-            for n in range(GT):
+            for n in range(LAST):
                 nc.sync.dma_start(
                     out=st[96:128, :].bitcast(I32).rearrange("p (g n w) -> p g n w", g=2, n=GT)[:, :, n, :],
                     in_=pack[32 * n : 32 * n + 32, :].bitcast(I32).rearrange("p (g w) -> p g w", g=2),
                 )
 
-        wsw = wsb[:].bitcast(F32).rearrange("p (r m e) -> p r m e", r=8, e=2)
-        wg = const.tile([P, 4 * HID], BF16, name="wg", align_bytes=64)
-        wgw = wg[:].bitcast(F32).rearrange("p (h e) -> p h e", e=2)
-        wq = const.tile([P, HID], U32, name="wq", align_bytes=64)
-        wsc = const.tile([P, HID], U8, name="wsc", align_bytes=64)
-
-        def prepare_weights(hf):
-            for rp in range(2 * hf, 2 * hf + 2):
-                wtp = mxp.tile([P, 512], F32, tag="mx")
-                for rl in range(2):
-                    for e in range(2):
-                        col = (rl * 2 + e) * P
-                        nc.tensor.transpose(wtp[:, col : col + P], wsw[:, rp * 2 + rl, :, e], ident[:])
-                dst = wgw[:, rp * 256 : (rp + 1) * 256, :].rearrange("p (r q) e -> p r q e", r=2)
-                src = wtp[:].rearrange("p (r e q) -> p r q e", r=2, e=2)
-                if rp == 0:
-                    nc.vector.tensor_copy(out=dst, in_=src)
-                else:
-                    nc.scalar.copy(out=dst, in_=src)
-            nc.vector.quantize_mx(
-                out=wq[:, hf * HALF : (hf + 1) * HALF].bitcast(FP8X4),
-                scales=wsc[:, hf * HALF : (hf + 1) * HALF],
-                in_=wg[:, hf * 4 * HALF : (hf + 1) * 4 * HALF],
+        def copy_last_edges(c):
+            nc.gpsimd.tensor_copy(
+                out=slots[c % N_SLOTS][96:128, :]
+                .bitcast(U32)
+                .rearrange("p (g n w) -> p g n w", g=2, n=GT)[:, :, LAST, :],
+                in_=packs[c % N_SLOTS][96:128, :].bitcast(U32).rearrange("p (g w) -> p g w", g=2),
             )
 
-        load_chunk(1)
-        fill_src(0)
-        spread_dst(0)
-        spread_dst(1)
+        wsw = wsb[:].bitcast(F32).rearrange("p (r m e) -> p r m e", r=8, e=2)
+        wgw = wg[:].bitcast(F32).rearrange("p (h e) -> p h e", e=2)
+        wbanks = {}
+
+        def transpose_weights(q):
+            wtp = mxp.tile([P, 512], F32, tag="mx")
+            for rl in range(2):
+                for e in range(2):
+                    col = (rl * 2 + e) * P
+                    nc.tensor.transpose(wtp[:, col : col + P], wsw[:, 2 * q + rl, :, e], ident[:])
+            wbanks[q] = wtp
+
+        def evacuate_weights(q):
+            nc.scalar.copy(
+                out=wgw[:, q * QUARTER : (q + 1) * QUARTER, :].rearrange("p (r q) e -> p r q e", r=2),
+                in_=wbanks[q][:].rearrange("p (r e q) -> p r q e", r=2, e=2),
+            )
+
+        def quantise_weights(q):
+            cols = slice(q * QUARTER, (q + 1) * QUARTER)
+            nc.vector.quantize_mx(
+                out=wq[:, cols].bitcast(FP8X4),
+                scales=wsc[:, cols],
+                in_=wg[:, 4 * q * QUARTER : 4 * (q + 1) * QUARTER],
+            )
+
+        def multiply(out_bank, tile_u8, lo, c0, n):
+            nc.tensor.matmul_mx(
+                out=out_bank,
+                lhsT=tile_u8[:, lo : lo + CODE_B].bitcast(FP8X4),
+                lhsT_scale=tile_u8[:, lo + CODE_B : lo + UNIT_B],
+                rhs=wq[:, c0 : c0 + n].bitcast(FP8X4),
+                rhs_scale=wsc[:, c0 : c0 + n],
+                start=True,
+                stop=True,
+            )
+
+        nrw = nr[:].bitcast(F32).rearrange("p (m e) -> p m e", e=2)
+        ntp = tpp.tile([P, 512], F32, tag="tp")
+        for e in range(2):
+            nc.tensor.transpose(ntp[:, e * P : (e + 1) * P], nrw[:, :, e], ident[:])
+        nc.vector.tensor_copy(
+            out=ntb[:].bitcast(F32).rearrange("p (q e) -> p q e", e=2),
+            in_=ntp[:, 0 : 2 * P].rearrange("p (e q) -> p q e", e=2),
+        )
+        nc.scalar.copy(
+            out=ntb4[:].bitcast(F32).rearrange("p (q r e) -> p q r e", r=REP, e=2),
+            in_=ntp[:, 0 : 2 * P]
+            .rearrange("p (e q) -> p q e", e=2)
+            .unsqueeze(2)
+            .to_broadcast([P, P, REP, 2]),
+        )
+        nc.vector.quantize_mx(
+            out=npack[:, 0:CODE_B].bitcast(FP8X4), scales=npack[:, CODE_B:UNIT_B], in_=ntb[:]
+        )
+        fill_rows(0, 34, 2, CODE_W, UNIT_W)
+        fill_rows(0, 48, 16, 0, UNIT_W)
+        fill_rows(0, 64, 32, 0, UNIT_W)
+        spread_group(0, scales=False)
+        fill_lead()
+        spread_codes(lead, 0, 2, codes_n[:, LAST, 0:2, :])
+        nc.vector.quantize_mx(out=n4c[:].bitcast(FP8X4), scales=n4s[:], in_=ntb4[:])
+        spread_scales(lead, 0, 2, scales_n[:, LAST, 0:2, :])
+
         transpose_edges(0)
-        evacuate_edges(0)
+        evacuate_edges(nc.scalar.copy, 0)
         quantise_edges(0)
+        nc.gpsimd.tensor_copy(out=lead[96:128, :].bitcast(U32), in_=packs[0][96:128, :].bitcast(U32))
         move_edges(0)
-        load_chunk(2)
-        fill_src(1)
-        prepare_weights(0)
-        prepare_weights(1)
-        spread_dst(2)
-        spread_dst(3)
-        transpose_edges(1)
-        for c in range(3, N_CHUNKS):
-            load_chunk(c)
-        fill_src(2)
+        spread_group(1, scales=False)
+        spread_group(0, codes=False)
+        spread_group(1, codes=False)
+        for q in range(2):
+            transpose_weights(q)
+            evacuate_weights(q)
+            quantise_weights(q)
+        for x in range(2, len(edges)):
+            load_edges(x)
+        fill_slot(1)
+        spread_group(2)
+        spread_group(3)
+        fill_slot(2)
+
+        o8v = o8[:].rearrange("p (g n h) -> p g n h", g=2, n=GT)
+        out_c0 = out_v[:, 0:CH, :].rearrange("p (g n) h -> p g n h", g=2)
+
+        def operand(gl, n):
+            if n == LAST:
+                return lead, gl * UNIT_B
+            return slots[0], (gl * GT + n) * UNIT_B
+
+        def leaky(bank, res, pair):
+            y = ypool.tile([P, HALF], F32, tag="y")
+            nc.scalar.activation(out=y[:], in_=bank[:], func=ACT.Copy, scale=NEG_SLOPE)
+            v, w = bank[:], y[:]
+            if pair:
+                v = v.rearrange("p (g h) -> p g h", g=2)
+                w = w.rearrange("p (g h) -> p g h", g=2)
+            nc.vector.tensor_tensor(out=res, in0=v, in1=w, op=ALU.max)
+
+        def pair_quarter(n, q):
+            mx = mxp.tile([P, HALF], F32, tag="mx")
+            for gl in range(2):
+                st, lo = operand(gl, n)
+                multiply(mx[:, gl * QUARTER : (gl + 1) * QUARTER], st, lo, q * QUARTER, QUARTER)
+            leaky(mx, o8v[:, :, n, q * QUARTER : (q + 1) * QUARTER], True)
+
+        def store_pair(n, hf):
+            cols = slice(hf * HALF, (hf + 1) * HALF)
+            nc.sync.dma_start(out=out_c0[:, :, n, cols], in_=o8v[:, :, n, cols])
+
+        pair_order = (LAST, 0, 1, 2)
+        for x in range(4):
+            n = pair_order[x]
+            pair_quarter(n, 0)
+            pair_quarter(n, 1)
+            store_pair(n, 0)
+            if x == 0:
+                transpose_weights(2)
+                evacuate_weights(2)
+            if x == 1:
+                quantise_weights(2)
+                transpose_weights(3)
+                evacuate_weights(3)
+                transpose_edges(1)
+            if x == 2:
+                quantise_weights(3)
+                evacuate_edges(nc.vector.tensor_copy, 1)
+        quantise_edges(1)
+        move_edges(1)
+        copy_last_edges(1)
+        for x in range(4):
+            n = pair_order[x]
+            for gl in range(2):
+                mx = mxp.tile([P, HALF], F32, tag="mx")
+                st, lo = operand(gl, n)
+                multiply(mx[:], st, lo, HALF, HALF)
+                leaky(mx, o8v[:, gl, n, HALF:HID], False)
+            store_pair(n, 1)
+            if x == 1:
+                transpose_edges(2)
+            if x == 2:
+                evacuate_edges(nc.vector.tensor_copy, 2)
+            if x == 3:
+                quantise_edges(2)
+                move_edges(2)
+                copy_last_edges(2)
+                spread_group(4)
+                spread_group(5)
 
         natural = [(t, hf) for t in range(GT) for hf in range(2)]
-
-        def store(o, g, t0, n):
-            nc.sync.dma_start(
-                out=out_v[:, g * GT + t0 : g * GT + t0 + n, :],
-                in_=o[:, t0 * HID : (t0 + n) * HID].rearrange("p (t h) -> p t h", t=n),
-            )
-
-        for g in range(N_GROUPS):
+        for g in range(2, N_GROUPS):
             c = g // 2
+            ahead = c + 2
             st = slots[c % N_SLOTS]
             o = opool.tile([P, GT * HID], F32, tag="o")
-            nxt = (g + 3) // 2 if (g == 0 or g % 2 == 1) and (g + 3) // 2 < N_CHUNKS else None
-            offload = g % 2 == 0 and g >= 2
-            per_store = 1 if g == 0 or g >= N_GROUPS - 2 else 2
+            fetch = ahead < N_CHUNKS
+            offload = g % 2 == 0
+            per_store = 1 if g < 4 or g >= N_GROUPS - 2 else 2
             order = [natural[-1]] + natural[:-1] if offload else natural
-            if g == 0:
-                spread_dst(2 * (c + 2))
-                spread_dst(2 * (c + 2) + 1)
+            if fetch and g % 2 == 0:
+                transpose_edges(ahead)
             seen = set()
             for j in range(2 * GT):
                 t, hf = order[j]
-                lo = ((g % 2) * GT + t) * UNIT_B
                 mx = mxp.tile([P, HALF], F32, tag="mx")
-                nc.tensor.matmul_mx(
-                    out=mx[:],
-                    lhsT=st[:, lo : lo + CODE_B].bitcast(FP8X4),
-                    lhsT_scale=st[:, lo + CODE_B : lo + UNIT_B],
-                    rhs=wq[:, hf * HALF : (hf + 1) * HALF].bitcast(FP8X4),
-                    rhs_scale=wsc[:, hf * HALF : (hf + 1) * HALF],
-                    start=True,
-                    stop=True,
-                )
+                multiply(mx[:], st, ((g % 2) * GT + t) * UNIT_B, hf * HALF, HALF)
                 col = t * HID + hf * HALF
                 res = o[:, col : col + HALF]
                 if offload and j == 0:
@@ -296,21 +399,22 @@ def tile_edge_update_only_pa_t_kernel(tc, node_fts, edge_fts, Wt, out):
                     )
                     nc.gpsimd.tensor_scalar(out=x[:], in0=x[:], scalar1=FLT_MAX, scalar2=0.0, op0=ALU.min, op1=ALU.max)
                     nc.gpsimd.tensor_tensor(out=res, in0=res, in1=x[:], op=ALU.add)
-                    if c + 2 < N_CHUNKS:
-                        spread_dst(2 * (c + 2))
-                        spread_dst(2 * (c + 2) + 1)
                 else:
-                    y = ypool.tile([P, HALF], F32, tag="y")
-                    nc.scalar.activation(out=y[:], in_=mx[:], func=ACT.Copy, scale=NEG_SLOPE)
-                    nc.vector.tensor_tensor(out=res, in0=mx[:], in1=y[:], op=ALU.max)
+                    leaky(mx, res, False)
+                if fetch and g % 2 == 0:
+                    if j == 2:
+                        evacuate_edges(nc.vector.tensor_copy, ahead)
+                    if j == 5:
+                        quantise_edges(ahead)
+                        move_edges(ahead)
+                        spread_group(2 * ahead)
                 seen.add((t, hf))
-                if j == 1 and nxt is not None:
-                    evacuate_edges(nxt)
                 t0 = t - t % per_store
                 if all((tt, hh) in seen for tt in range(t0, t0 + per_store) for hh in range(2)):
-                    store(o, g, t0, per_store)
-                if j == (3 if g == 0 else 7) and nxt is not None:
-                    quantise_edges(nxt)
-                    move_edges(nxt)
-            if g % 2 == 0 and c + 2 < N_CHUNKS:
-                transpose_edges(c + 2)
+                    nc.sync.dma_start(
+                        out=out_v[:, g * GT + t0 : g * GT + t0 + per_store, :],
+                        in_=o[:, t0 * HID : (t0 + per_store) * HID].rearrange("p (t h) -> p t h", t=per_store),
+                    )
+            if fetch and g % 2 == 1:
+                copy_last_edges(ahead)
+                spread_group(2 * ahead + 1)

@@ -34,8 +34,10 @@ UNIT_B = CODE_B + SCALE_B
 UNIT_W = UNIT_B // 4
 CODE_W = CODE_B // 4
 SCALE_W = SCALE_B // 4
-DST_P = NODE_IN // 4
-DST_SCALE_P = 34
+SRC_P = NODE_IN // 4
+SRC_SCALE_P = 34
+N_SRC = P * CH // N_NODE
+N_DST = N_NODE // CH
 REP = 4
 LAST = GT - 1
 Y_BUFS = 8
@@ -46,10 +48,10 @@ FLOPS = 2 * 2 * N_NODE * N_NODE * D_IN * HID
 
 def tile_edge_update_only_pa_t_kernel(tc, node_fts, edge_fts, Wt, out):
     nc = tc.nc
-    edge_v = edge_fts.rearrange("b (i k) f -> (b i) k f", k=N_NODE)
-    out_v = out.rearrange("b (i k) h -> (b i) k h", k=N_NODE)
+    edge_v = edge_fts.rearrange("b (c p t) f -> p (b c) (t f)", p=P, t=CH)
+    out_v = out.rearrange("b (c p t) h -> (b c) p t h", p=P, t=CH)
     node_rows = node_fts.flatten_outer_dims()
-    w_v = Wt.rearrange("(r p) k -> p r k", p=P)
+    w_v = Wt.rearrange("(q p r) k -> p q (r k)", p=P, r=2)
 
     with ExitStack() as ctx:
         const = ctx.enter_context(tc.tile_pool(name="const", bufs=1))
@@ -87,89 +89,77 @@ def tile_edge_update_only_pa_t_kernel(tc, node_fts, edge_fts, Wt, out):
         wsc = const.tile([P, HID], U8, name="wsc", align_bytes=64)
         o8 = const.tile([P, CH * HID], F32, name="o8")
 
-        wsb3 = wsb[:].rearrange("p (r k) -> p r k", r=8)
-
-        def load_weights(r0, n):
-            rows = slice(r0, r0 + n)
-            nc.sync.dma_start(out=wsb3[:, rows, 0:NODE_IN], in_=w_v[:, rows, NODE_IN : 2 * NODE_IN])
-            nc.sync.dma_start(out=wsb3[:, rows, NODE_IN : 2 * NODE_IN], in_=w_v[:, rows, 0:NODE_IN])
-            nc.sync.dma_start(out=wsb3[:, rows, 2 * NODE_IN :], in_=w_v[:, rows, 2 * NODE_IN :])
+        def load_weights(q, n):
+            nc.sync.dma_start(
+                out=wsb[:].rearrange("p (q x) -> p q x", q=4)[:, q : q + n, :], in_=w_v[:, q : q + n, :]
+            )
 
         def load_edges(x):
             c, n, ec = edges[x]
-            nc.sync.dma_start(
-                out=ec[:].rearrange("p (k f) -> p k f", f=EDGE_IN),
-                in_=edge_v[:, c * CH : (c + n) * CH, :],
-            )
+            nc.sync.dma_start(out=ec[:].rearrange("p (c x) -> p c x", c=n), in_=edge_v[:, c : c + n, :])
 
         nc.sync.dma_start(
             out=nr[:, 0 : 2 * NODE_IN].rearrange("p (s f) -> p s f", s=2),
             in_=node_rows.unsqueeze(1).to_broadcast([P, 2, NODE_IN]),
         )
         load_edges(0)
-        load_weights(0, 2)
+        load_weights(0, 1)
+        load_weights(1, 1)
         load_weights(2, 2)
-        load_weights(4, 4)
         load_edges(1)
 
         make_identity(nc, ident[:])
         nc.vector.memset(nr[:, 2 * NODE_IN : D_IN], 0.0)
         nc.vector.memset(npack[:, CODE_B:UNIT_B].bitcast(I32), 0)
         nc.vector.memset(n4s[:].bitcast(I32), 0)
-        nc.vector.memset(slots[0][:].bitcast(I32), 0)
         for pt in packs:
             nc.vector.memset(pt[:].bitcast(I32), 0)
 
-        def fill_lead():
-            for p0 in (32, 64):
-                nc.vector.tensor_copy(
-                    out=lead[p0 : p0 + 32, :].bitcast(I32).rearrange("p (t w) -> p t w", t=2),
-                    in_=npack[p0 : p0 + 32, :].bitcast(I32).unsqueeze(1).to_broadcast([32, 2, UNIT_W]),
-                )
+        dcodes = npack[:, 0:CODE_B].bitcast(I32).rearrange("p (b t j) -> p b t j", b=2, t=CH)
+        dscales = npack[:, CODE_B:UNIT_B].bitcast(I32).rearrange("p (b t j) -> p b t j", b=2, t=CH)
 
-        def fill_rows(s, p0, n, lo, hi):
-            nc.sync.dma_start(
-                out=slots[s][p0 : p0 + n, :].bitcast(I32).rearrange("p (t w) -> p t w", t=CH)[:, :, lo:hi],
-                in_=npack[p0 : p0 + n, 4 * lo : 4 * hi].bitcast(I32).unsqueeze(1).to_broadcast([n, CH, hi - lo]),
+        def units(dst, p0, n):
+            return dst[p0 : p0 + n, :].bitcast(I32).rearrange("p (t w) -> p t w", w=UNIT_W)
+
+        def fill_dst_codes(engine, dst, p0, src):
+            nt = src.shape[1]
+            engine.tensor_copy(
+                out=units(dst, p0, 32)[:, :, 0:CODE_W].rearrange("p t (i j) -> p t i j", j=N_DST),
+                in_=src.unsqueeze(2).to_broadcast([32, nt, N_SRC, N_DST]),
             )
 
-        def fill_slot(s):
-            for p0 in (32, 64):
-                nc.gpsimd.tensor_copy(
-                    out=slots[s][p0 : p0 + 32, :].bitcast(U32).rearrange("p (t w) -> p t w", t=CH),
-                    in_=npack[p0 : p0 + 32, :].bitcast(U32).unsqueeze(1).to_broadcast([32, CH, UNIT_W]),
-                )
+        def fill_dst_scales(engine, dst, p0, src):
+            nt = src.shape[1]
+            engine.tensor_copy(
+                out=units(dst, p0, 32)[:, :, CODE_W:UNIT_W].rearrange("p t (i j) -> p t i j", j=N_DST // 4),
+                in_=src.unsqueeze(2).to_broadcast([32, nt, N_SRC, N_DST // 4]),
+            )
 
-        def spread_codes(dst, t0, nt, src):
+        scodes = n4c[:].bitcast(I32).rearrange("p (c i r) -> p c i r", i=N_SRC, r=REP)
+        sscales = n4s[:].bitcast(I32).rearrange("p (c i) -> p c i", i=N_SRC)
+
+        def spread_src(dst, c, nt):
+            spread_src_codes(dst, c, nt)
+            spread_src_scales(dst, c, nt)
+
+        def spread_src_codes(dst, c, nt):
             nc.gpsimd.tensor_copy(
-                out=dst[0:DST_P, t0 * UNIT_B : (t0 + nt) * UNIT_B]
-                .bitcast(U32)
-                .rearrange("p (t w) -> p t w", t=nt)[:, :, 0:CODE_W]
-                .rearrange("p t (b i) -> p t b i", b=2),
-                in_=src.unsqueeze(3).to_broadcast([DST_P, nt, 2, N_NODE]),
+                out=units(dst, 0, SRC_P)[:, :, 0:CODE_W].rearrange("p t (i j) -> p t i j", j=N_DST),
+                in_=scodes[0:SRC_P, c, :, 0:1].unsqueeze(1).to_broadcast([SRC_P, nt, N_SRC, N_DST]),
             )
 
-        def spread_scales(dst, t0, nt, src):
+        def spread_src_scales(dst, c, nt):
             nc.gpsimd.tensor_copy(
-                out=dst[0:DST_SCALE_P, t0 * UNIT_B : (t0 + nt) * UNIT_B]
-                .bitcast(U32)
-                .rearrange("p (t w) -> p t w", t=nt)[:, :, CODE_W:UNIT_W]
-                .rearrange("p t (b i) -> p t b i", b=2),
-                in_=src.unsqueeze(3).to_broadcast([DST_SCALE_P, nt, 2, SCALE_W // 2]),
+                out=units(dst, 0, SRC_SCALE_P)[:, :, CODE_W:UNIT_W].rearrange("p t (i j) -> p t i j", j=N_DST // 4),
+                in_=sscales[0:SRC_SCALE_P, c, :].unsqueeze(1).unsqueeze(3).to_broadcast(
+                    [SRC_SCALE_P, nt, N_SRC, N_DST // 4]
+                ),
             )
 
-        codes_k = npack[0:DST_P, 0:CODE_B].bitcast(U32).rearrange("p (b k) -> p k b", b=2)
-        scales_k = n4s[0:DST_SCALE_P, :].bitcast(U32).rearrange("p (b k) -> p k b", b=2)
-        codes_n = npack[0:DST_P, 0:CODE_B].bitcast(U32).rearrange("p (b g n) -> p n g b", b=2, n=GT)
-        scales_n = n4s[0:DST_SCALE_P, :].bitcast(U32).rearrange("p (b g n) -> p n g b", b=2, n=GT)
-
-        def spread_group(g, codes=True, scales=True):
-            st = slots[(g // 2) % N_SLOTS]
-            t0 = (g % 2) * GT
-            if codes:
-                spread_codes(st, t0, GT, codes_k[:, g * GT : (g + 1) * GT, :])
-            if scales:
-                spread_scales(st, t0, GT, scales_k[:, g * GT : (g + 1) * GT, :])
+        def fill_dst(s, b):
+            for p0 in (32, 64):
+                fill_dst_codes(nc.gpsimd, slots[s], p0, dcodes[p0 : p0 + 32, b, :, :])
+                fill_dst_scales(nc.gpsimd, slots[s], p0, dscales[p0 : p0 + 32, b, :, :])
 
         banks = {}
         staged = {}
@@ -236,8 +226,8 @@ def tile_edge_update_only_pa_t_kernel(tc, node_fts, edge_fts, Wt, out):
 
         def evacuate_weights(q):
             nc.scalar.copy(
-                out=wgw[:, q * QUARTER : (q + 1) * QUARTER, :].rearrange("p (r q) e -> p r q e", r=2),
-                in_=wbanks[q][:].rearrange("p (r e q) -> p r q e", r=2, e=2),
+                out=wgw[:, q * QUARTER : (q + 1) * QUARTER, :].rearrange("p (m r) e -> p m r e", r=2),
+                in_=wbanks[q][:].rearrange("p (r e m) -> p m r e", r=2, e=2),
             )
 
         def quantise_weights(q):
@@ -263,10 +253,11 @@ def tile_edge_update_only_pa_t_kernel(tc, node_fts, edge_fts, Wt, out):
         ntp = tpp.tile([P, 512], F32, tag="tp")
         for e in range(2):
             nc.tensor.transpose(ntp[:, e * P : (e + 1) * P], nrw[:, :, e], ident[:])
-        nc.vector.tensor_copy(
-            out=ntb[:].bitcast(F32).rearrange("p (q e) -> p q e", e=2),
-            in_=ntp[:, 0 : 2 * P].rearrange("p (e q) -> p q e", e=2),
-        )
+        for b in range(2):
+            nc.vector.tensor_copy(
+                out=ntb[:].bitcast(F32).rearrange("p (b t j e) -> p b t j e", b=2, t=CH, e=2)[:, b],
+                in_=ntp[:, 0 : 2 * P].rearrange("p (e b j t) -> p b t j e", e=2, b=2, t=CH)[:, b],
+            )
         nc.scalar.copy(
             out=ntb4[:].bitcast(F32).rearrange("p (q r e) -> p q r e", r=REP, e=2),
             in_=ntp[:, 0 : 2 * P]
@@ -277,36 +268,33 @@ def tile_edge_update_only_pa_t_kernel(tc, node_fts, edge_fts, Wt, out):
         nc.vector.quantize_mx(
             out=npack[:, 0:CODE_B].bitcast(FP8X4), scales=npack[:, CODE_B:UNIT_B], in_=ntb[:]
         )
-        fill_rows(0, 34, 2, CODE_W, UNIT_W)
-        fill_rows(0, 48, 16, 0, UNIT_W)
-        fill_rows(0, 64, 32, 0, UNIT_W)
-        spread_group(0, scales=False)
-        fill_lead()
-        spread_codes(lead, 0, 2, codes_n[:, LAST, 0:2, :])
+        for p0 in (32, 64):
+            fill_dst_codes(nc.gpsimd, lead, p0, dcodes[p0 : p0 + 32, 0, LAST:CH:GT, :])
+            fill_dst_scales(nc.gpsimd, lead, p0, dscales[p0 : p0 + 32, 0, LAST:CH:GT, :])
+        fill_dst_codes(nc.vector, slots[0], 64, dcodes[64:96, 0, :, :])
         nc.vector.quantize_mx(out=n4c[:].bitcast(FP8X4), scales=n4s[:], in_=ntb4[:])
-        spread_scales(lead, 0, 2, scales_n[:, LAST, 0:2, :])
+        spread_src(lead, 0, 2)
+        fill_dst_codes(nc.vector, slots[0], 32, dcodes[32:64, 0, :, :])
 
         transpose_edges(0)
         evacuate_edges(nc.scalar.copy, 0)
         quantise_edges(0)
         nc.gpsimd.tensor_copy(out=lead[96:128, :].bitcast(U32), in_=packs[0][96:128, :].bitcast(U32))
         move_edges(0)
-        spread_group(1, scales=False)
-        spread_group(0, codes=False)
-        spread_group(1, codes=False)
+        for p0 in (32, 64):
+            fill_dst_scales(nc.vector, slots[0], p0, dscales[p0 : p0 + 32, 0, :, :])
+        spread_src(slots[0], 0, CH)
         for q in range(2):
             transpose_weights(q)
             evacuate_weights(q)
             quantise_weights(q)
         for x in range(2, len(edges)):
             load_edges(x)
-        fill_slot(1)
-        spread_group(2)
-        spread_group(3)
-        fill_slot(2)
+        fill_dst(1, 0)
+        spread_src(slots[1], 1, CH)
 
         o8v = o8[:].rearrange("p (g n h) -> p g n h", g=2, n=GT)
-        out_c0 = out_v[:, 0:CH, :].rearrange("p (g n) h -> p g n h", g=2)
+        out_c0 = out_v[0].rearrange("p (g n) h -> p g n h", g=2)
 
         def operand(gl, n):
             if n == LAST:
@@ -353,6 +341,8 @@ def tile_edge_update_only_pa_t_kernel(tc, node_fts, edge_fts, Wt, out):
         quantise_edges(1)
         move_edges(1)
         copy_last_edges(1)
+        fill_dst(2, 0)
+        spread_src(slots[2], 2, CH)
         for x in range(4):
             n = pair_order[x]
             for gl in range(2):
@@ -369,8 +359,6 @@ def tile_edge_update_only_pa_t_kernel(tc, node_fts, edge_fts, Wt, out):
                 quantise_edges(2)
                 move_edges(2)
                 copy_last_edges(2)
-                spread_group(4)
-                spread_group(5)
 
         natural = [(t, hf) for t in range(GT) for hf in range(2)]
         for g in range(2, N_GROUPS):
@@ -402,19 +390,20 @@ def tile_edge_update_only_pa_t_kernel(tc, node_fts, edge_fts, Wt, out):
                 else:
                     leaky(mx, res, False)
                 if fetch and g % 2 == 0:
+                    if j == 0 and ahead >= N_CHUNKS // 2 and ahead < N_CHUNKS // 2 + N_SLOTS:
+                        fill_dst(ahead % N_SLOTS, 1)
                     if j == 2:
                         evacuate_edges(nc.vector.tensor_copy, ahead)
                     if j == 5:
                         quantise_edges(ahead)
                         move_edges(ahead)
-                        spread_group(2 * ahead)
+                        copy_last_edges(ahead)
                 seen.add((t, hf))
                 t0 = t - t % per_store
                 if all((tt, hh) in seen for tt in range(t0, t0 + per_store) for hh in range(2)):
                     nc.sync.dma_start(
-                        out=out_v[:, g * GT + t0 : g * GT + t0 + per_store, :],
+                        out=out_v[c][:, (g % 2) * GT + t0 : (g % 2) * GT + t0 + per_store, :],
                         in_=o[:, t0 * HID : (t0 + per_store) * HID].rearrange("p (t h) -> p t h", t=per_store),
                     )
             if fetch and g % 2 == 1:
-                copy_last_edges(ahead)
-                spread_group(2 * ahead + 1)
+                spread_src(slots[ahead % N_SLOTS], ahead, CH)

@@ -107,6 +107,7 @@ def tile_edge_update_only_pa_t_kernel(tc, node_fts, edge_fts, Wt, out):
         load_weights(1, 1)
         load_weights(2, 2)
         load_edges(1)
+        load_edges(2)
 
         make_identity(nc, ident[:])
         nc.vector.memset(nr[:, 2 * NODE_IN : D_IN], 0.0)
@@ -288,7 +289,7 @@ def tile_edge_update_only_pa_t_kernel(tc, node_fts, edge_fts, Wt, out):
             transpose_weights(q)
             evacuate_weights(q)
             quantise_weights(q)
-        for x in range(2, len(edges)):
+        for x in range(3, len(edges)):
             load_edges(x)
         fill_dst(1, 0)
         spread_src(slots[1], 1, CH)
@@ -328,21 +329,19 @@ def tile_edge_update_only_pa_t_kernel(tc, node_fts, edge_fts, Wt, out):
             pair_quarter(n, 1)
             store_pair(n, 0)
             if x == 0:
-                transpose_weights(2)
-                evacuate_weights(2)
+                for q in (2, 3):
+                    transpose_weights(q)
+                    evacuate_weights(q)
+                    quantise_weights(q)
             if x == 1:
-                quantise_weights(2)
-                transpose_weights(3)
-                evacuate_weights(3)
                 transpose_edges(1)
+                evacuate_edges(nc.scalar.copy, 1)
             if x == 2:
-                quantise_weights(3)
-                evacuate_edges(nc.vector.tensor_copy, 1)
-        quantise_edges(1)
-        move_edges(1)
-        copy_last_edges(1)
-        fill_dst(2, 0)
-        spread_src(slots[2], 2, CH)
+                quantise_edges(1)
+                move_edges(1)
+                copy_last_edges(1)
+                fill_dst(2, 0)
+                spread_src(slots[2], 2, CH)
         for x in range(4):
             n = pair_order[x]
             for gl in range(2):
@@ -351,11 +350,11 @@ def tile_edge_update_only_pa_t_kernel(tc, node_fts, edge_fts, Wt, out):
                 multiply(mx[:], st, lo, HALF, HALF)
                 leaky(mx, o8v[:, gl, n, HALF:HID], False)
             store_pair(n, 1)
-            if x == 1:
+            if x == 0:
                 transpose_edges(2)
+            if x == 1:
+                evacuate_edges(nc.scalar.copy, 2)
             if x == 2:
-                evacuate_edges(nc.vector.tensor_copy, 2)
-            if x == 3:
                 quantise_edges(2)
                 move_edges(2)
                 copy_last_edges(2)
@@ -363,23 +362,24 @@ def tile_edge_update_only_pa_t_kernel(tc, node_fts, edge_fts, Wt, out):
         natural = [(t, hf) for t in range(GT) for hf in range(2)]
         for g in range(2, N_GROUPS):
             c = g // 2
+            odd = g % 2
             ahead = c + 2
             st = slots[c % N_SLOTS]
             o = opool.tile([P, GT * HID], F32, tag="o")
-            fetch = ahead < N_CHUNKS
-            offload = g % 2 == 0
+            fetch = ahead < N_CHUNKS and not odd
+            past = None if odd else 0
             per_store = 1 if g < 4 or g >= N_GROUPS - 2 else 2
-            order = [natural[-1]] + natural[:-1] if offload else natural
-            if fetch and g % 2 == 0:
+            order = natural if odd else [natural[-1]] + natural[:-1]
+            if fetch:
                 transpose_edges(ahead)
             seen = set()
             for j in range(2 * GT):
                 t, hf = order[j]
                 mx = mxp.tile([P, HALF], F32, tag="mx")
-                multiply(mx[:], st, ((g % 2) * GT + t) * UNIT_B, hf * HALF, HALF)
+                multiply(mx[:], st, (odd * GT + t) * UNIT_B, hf * HALF, HALF)
                 col = t * HID + hf * HALF
                 res = o[:, col : col + HALF]
-                if offload and j == 0:
+                if j == past:
                     nc.scalar.copy(out=res, in_=mx[:])
                     x = xpool.tile([P, HALF], F32, tag="x")
                     nc.gpsimd.tensor_scalar(
@@ -389,21 +389,25 @@ def tile_edge_update_only_pa_t_kernel(tc, node_fts, edge_fts, Wt, out):
                     nc.gpsimd.tensor_tensor(out=res, in0=res, in1=x[:], op=ALU.add)
                 else:
                     leaky(mx, res, False)
-                if fetch and g % 2 == 0:
-                    if j == 0 and ahead >= N_CHUNKS // 2 and ahead < N_CHUNKS // 2 + N_SLOTS:
+                if fetch and j == 2:
+                    evacuate_edges(nc.vector.tensor_copy, ahead)
+                if fetch and j == 6:
+                    quantise_edges(ahead)
+                    move_edges(ahead)
+                    copy_last_edges(ahead)
+                    if N_CHUNKS // 2 <= ahead < N_CHUNKS // 2 + N_SLOTS:
                         fill_dst(ahead % N_SLOTS, 1)
-                    if j == 2:
-                        evacuate_edges(nc.vector.tensor_copy, ahead)
-                    if j == 5:
-                        quantise_edges(ahead)
-                        move_edges(ahead)
-                        copy_last_edges(ahead)
+                    spread_src(slots[ahead % N_SLOTS], ahead, CH)
                 seen.add((t, hf))
+                row = odd * GT + t
+                if g == N_GROUPS - 1 and t == GT - 1:
+                    nc.sync.dma_start(
+                        out=out_v[c][:, row : row + 1, hf * HALF : (hf + 1) * HALF], in_=res.unsqueeze(1)
+                    )
+                    continue
                 t0 = t - t % per_store
                 if all((tt, hh) in seen for tt in range(t0, t0 + per_store) for hh in range(2)):
                     nc.sync.dma_start(
-                        out=out_v[c][:, (g % 2) * GT + t0 : (g % 2) * GT + t0 + per_store, :],
+                        out=out_v[c][:, odd * GT + t0 : odd * GT + t0 + per_store, :],
                         in_=o[:, t0 * HID : (t0 + per_store) * HID].rearrange("p (t h) -> p t h", t=per_store),
                     )
-            if fetch and g % 2 == 1:
-                spread_src(slots[ahead % N_SLOTS], ahead, CH)

@@ -83,11 +83,9 @@ def tile_edge_update_only_pa_t_kernel(tc, node_fts, edge_fts, Wt, out):
         for s in range(N_SLOTS):
             st = const.tile([P, CH * UNIT_B], U8, name="st%d" % s, align_bytes=64)
             slots.append(st)
-        lead = const.tile([P, 2 * UNIT_B], U8, name="lead", align_bytes=64)
         wg = const.tile([P, 4 * HID], BF16, name="wg", align_bytes=64)
         wq = const.tile([P, HID], U32, name="wq", align_bytes=64)
         wsc = const.tile([P, HID], U8, name="wsc", align_bytes=64)
-        o8 = const.tile([P, CH * HID], F32, name="o8")
 
         def load_weights(q, n):
             nc.sync.dma_start(
@@ -107,7 +105,6 @@ def tile_edge_update_only_pa_t_kernel(tc, node_fts, edge_fts, Wt, out):
         load_weights(1, 1)
         load_weights(2, 2)
         load_edges(1)
-        load_edges(2)
 
         make_identity(nc, ident[:])
         nc.vector.memset(nr[:, 2 * NODE_IN : D_IN], 0.0)
@@ -140,17 +137,17 @@ def tile_edge_update_only_pa_t_kernel(tc, node_fts, edge_fts, Wt, out):
         sscales = n4s[:].bitcast(I32).rearrange("p (c i) -> p c i", i=N_SRC)
 
         def spread_src(dst, c, nt):
-            spread_src_codes(dst, c, nt)
-            spread_src_scales(dst, c, nt)
+            spread_src_codes(nc.gpsimd, dst, c, nt)
+            spread_src_scales(nc.gpsimd, dst, c, nt)
 
-        def spread_src_codes(dst, c, nt):
-            nc.gpsimd.tensor_copy(
+        def spread_src_codes(engine, dst, c, nt):
+            engine.tensor_copy(
                 out=units(dst, 0, SRC_P)[:, :, 0:CODE_W].rearrange("p t (i j) -> p t i j", j=N_DST),
                 in_=scodes[0:SRC_P, c, :, 0:1].unsqueeze(1).to_broadcast([SRC_P, nt, N_SRC, N_DST]),
             )
 
-        def spread_src_scales(dst, c, nt):
-            nc.gpsimd.tensor_copy(
+        def spread_src_scales(engine, dst, c, nt):
+            engine.tensor_copy(
                 out=units(dst, 0, SRC_SCALE_P)[:, :, CODE_W:UNIT_W].rearrange("p t (i j) -> p t i j", j=N_DST // 4),
                 in_=sscales[0:SRC_SCALE_P, c, :].unsqueeze(1).unsqueeze(3).to_broadcast(
                     [SRC_SCALE_P, nt, N_SRC, N_DST // 4]
@@ -199,7 +196,7 @@ def tile_edge_update_only_pa_t_kernel(tc, node_fts, edge_fts, Wt, out):
         def move_edges(c):
             st = slots[c % N_SLOTS]
             pack = packs[c % N_SLOTS]
-            for n in range(LAST):
+            for n in range(GT if c == 0 else LAST):
                 nc.sync.dma_start(
                     out=st[96:128, :].bitcast(I32).rearrange("p (g n w) -> p g n w", g=2, n=GT)[:, :, n, :],
                     in_=pack[32 * n : 32 * n + 32, :].bitcast(I32).rearrange("p (g w) -> p g w", g=2),
@@ -259,6 +256,13 @@ def tile_edge_update_only_pa_t_kernel(tc, node_fts, edge_fts, Wt, out):
                 out=ntb[:].bitcast(F32).rearrange("p (b t j e) -> p b t j e", b=2, t=CH, e=2)[:, b],
                 in_=ntp[:, 0 : 2 * P].rearrange("p (e b j t) -> p b t j e", e=2, b=2, t=CH)[:, b],
             )
+        nc.vector.quantize_mx(
+            out=npack[:, 0:CODE_B].bitcast(FP8X4), scales=npack[:, CODE_B:UNIT_B], in_=ntb[:]
+        )
+        fill_dst_codes(nc.vector, slots[0], 64, dcodes[64:96, 0, :, :])
+
+        transpose_edges(0)
+        evacuate_edges(nc.scalar.copy, 0)
         nc.scalar.copy(
             out=ntb4[:].bitcast(F32).rearrange("p (q r e) -> p q r e", r=REP, e=2),
             in_=ntp[:, 0 : 2 * P]
@@ -266,111 +270,50 @@ def tile_edge_update_only_pa_t_kernel(tc, node_fts, edge_fts, Wt, out):
             .unsqueeze(2)
             .to_broadcast([P, P, REP, 2]),
         )
-        nc.vector.quantize_mx(
-            out=npack[:, 0:CODE_B].bitcast(FP8X4), scales=npack[:, CODE_B:UNIT_B], in_=ntb[:]
-        )
-        for p0 in (32, 64):
-            fill_dst_codes(nc.gpsimd, lead, p0, dcodes[p0 : p0 + 32, 0, LAST:CH:GT, :])
-            fill_dst_scales(nc.gpsimd, lead, p0, dscales[p0 : p0 + 32, 0, LAST:CH:GT, :])
-        fill_dst_codes(nc.vector, slots[0], 64, dcodes[64:96, 0, :, :])
-        nc.vector.quantize_mx(out=n4c[:].bitcast(FP8X4), scales=n4s[:], in_=ntb4[:])
-        spread_src(lead, 0, 2)
-        fill_dst_codes(nc.vector, slots[0], 32, dcodes[32:64, 0, :, :])
-
-        transpose_edges(0)
-        evacuate_edges(nc.scalar.copy, 0)
         quantise_edges(0)
-        nc.gpsimd.tensor_copy(out=lead[96:128, :].bitcast(U32), in_=packs[0][96:128, :].bitcast(U32))
         move_edges(0)
-        for p0 in (32, 64):
-            fill_dst_scales(nc.vector, slots[0], p0, dscales[p0 : p0 + 32, 0, :, :])
-        spread_src(slots[0], 0, CH)
-        for q in range(2):
+        fill_dst_codes(nc.vector, slots[0], 32, dcodes[32:64, 0, :, :])
+        nc.vector.quantize_mx(out=n4c[:].bitcast(FP8X4), scales=n4s[:], in_=ntb4[:])
+        for q in range(4):
             transpose_weights(q)
             evacuate_weights(q)
+        quantise_weights(0)
+        for p0 in (64, 32):
+            fill_dst_scales(nc.vector, slots[0], p0, dscales[p0 : p0 + 32, 0, :, :])
+        spread_src_codes(nc.vector, slots[0], 0, CH)
+        spread_src_scales(nc.vector, slots[0], 0, CH)
+        for q in range(1, 4):
             quantise_weights(q)
+        transpose_edges(1)
+        load_edges(2)
+        for s in (1, 2):
+            for p0 in (64, 32):
+                nc.sync.dma_start(
+                    out=slots[s][p0 : p0 + 32, :].bitcast(I32), in_=slots[0][p0 : p0 + 32, :].bitcast(I32)
+                )
         for x in range(3, len(edges)):
             load_edges(x)
-        fill_dst(1, 0)
-        spread_src(slots[1], 1, CH)
 
-        o8v = o8[:].rearrange("p (g n h) -> p g n h", g=2, n=GT)
-        out_c0 = out_v[0].rearrange("p (g n) h -> p g n h", g=2)
-
-        def operand(gl, n):
-            if n == LAST:
-                return lead, gl * UNIT_B
-            return slots[0], (gl * GT + n) * UNIT_B
-
-        def leaky(bank, res, pair):
+        def leaky(bank, res):
             y = ypool.tile([P, HALF], F32, tag="y")
             nc.scalar.activation(out=y[:], in_=bank[:], func=ACT.Copy, scale=NEG_SLOPE)
-            v, w = bank[:], y[:]
-            if pair:
-                v = v.rearrange("p (g h) -> p g h", g=2)
-                w = w.rearrange("p (g h) -> p g h", g=2)
-            nc.vector.tensor_tensor(out=res, in0=v, in1=w, op=ALU.max)
-
-        def pair_quarter(n, q):
-            mx = mxp.tile([P, HALF], F32, tag="mx")
-            for gl in range(2):
-                st, lo = operand(gl, n)
-                multiply(mx[:, gl * QUARTER : (gl + 1) * QUARTER], st, lo, q * QUARTER, QUARTER)
-            leaky(mx, o8v[:, :, n, q * QUARTER : (q + 1) * QUARTER], True)
-
-        def store_pair(n, hf):
-            cols = slice(hf * HALF, (hf + 1) * HALF)
-            nc.sync.dma_start(out=out_c0[:, :, n, cols], in_=o8v[:, :, n, cols])
-
-        pair_order = (LAST, 0, 1, 2)
-        for x in range(4):
-            n = pair_order[x]
-            pair_quarter(n, 0)
-            pair_quarter(n, 1)
-            store_pair(n, 0)
-            if x == 0:
-                for q in (2, 3):
-                    transpose_weights(q)
-                    evacuate_weights(q)
-                    quantise_weights(q)
-            if x == 1:
-                transpose_edges(1)
-                evacuate_edges(nc.scalar.copy, 1)
-            if x == 2:
-                quantise_edges(1)
-                move_edges(1)
-                copy_last_edges(1)
-                fill_dst(2, 0)
-                spread_src(slots[2], 2, CH)
-        for x in range(4):
-            n = pair_order[x]
-            for gl in range(2):
-                mx = mxp.tile([P, HALF], F32, tag="mx")
-                st, lo = operand(gl, n)
-                multiply(mx[:], st, lo, HALF, HALF)
-                leaky(mx, o8v[:, gl, n, HALF:HID], False)
-            store_pair(n, 1)
-            if x == 0:
-                transpose_edges(2)
-            if x == 1:
-                evacuate_edges(nc.scalar.copy, 2)
-            if x == 2:
-                quantise_edges(2)
-                move_edges(2)
-                copy_last_edges(2)
+            nc.vector.tensor_tensor(out=res, in0=bank[:], in1=y[:], op=ALU.max)
 
         natural = [(t, hf) for t in range(GT) for hf in range(2)]
-        for g in range(2, N_GROUPS):
+        for g in range(N_GROUPS):
             c = g // 2
             odd = g % 2
-            ahead = c + 2
             st = slots[c % N_SLOTS]
             o = opool.tile([P, GT * HID], F32, tag="o")
-            fetch = ahead < N_CHUNKS and not odd
-            past = None if odd else 0
-            per_store = 1 if g < 4 or g >= N_GROUPS - 2 else 2
-            order = natural if odd else [natural[-1]] + natural[:-1]
-            if fetch:
+            ahead, copy_at, quantise_at, copier = None, 2, 6, nc.vector.tensor_copy
+            if g < 2:
+                ahead, copy_at, quantise_at, copier = g + 1, 1, 3, nc.scalar.copy
+            elif not odd and c + 2 < N_CHUNKS:
+                ahead = c + 2
+            past_vector = not odd and g >= 2
+            per_store = 1 if g < 3 or g >= N_GROUPS - 2 else 2
+            order = [natural[-1]] + natural[:-1] if past_vector else natural
+            if ahead is not None and g > 0:
                 transpose_edges(ahead)
             seen = set()
             for j in range(2 * GT):
@@ -379,7 +322,7 @@ def tile_edge_update_only_pa_t_kernel(tc, node_fts, edge_fts, Wt, out):
                 multiply(mx[:], st, (odd * GT + t) * UNIT_B, hf * HALF, HALF)
                 col = t * HID + hf * HALF
                 res = o[:, col : col + HALF]
-                if j == past:
+                if past_vector and j == 0:
                     nc.scalar.copy(out=res, in_=mx[:])
                     x = xpool.tile([P, HALF], F32, tag="x")
                     nc.gpsimd.tensor_scalar(
@@ -388,10 +331,10 @@ def tile_edge_update_only_pa_t_kernel(tc, node_fts, edge_fts, Wt, out):
                     nc.gpsimd.tensor_scalar(out=x[:], in0=x[:], scalar1=FLT_MAX, scalar2=0.0, op0=ALU.min, op1=ALU.max)
                     nc.gpsimd.tensor_tensor(out=res, in0=res, in1=x[:], op=ALU.add)
                 else:
-                    leaky(mx, res, False)
-                if fetch and j == 2:
-                    evacuate_edges(nc.vector.tensor_copy, ahead)
-                if fetch and j == 6:
+                    leaky(mx, res)
+                if ahead is not None and j == copy_at:
+                    evacuate_edges(copier, ahead)
+                if ahead is not None and j == quantise_at:
                     quantise_edges(ahead)
                     move_edges(ahead)
                     copy_last_edges(ahead)

@@ -34,10 +34,8 @@ UNIT_B = CODE_B + SCALE_B
 UNIT_W = UNIT_B // 4
 CODE_W = CODE_B // 4
 SCALE_W = SCALE_B // 4
-SRC_P = NODE_IN // 4
-SRC_SCALE_P = 34
-N_SRC = P * CH // N_NODE
-N_DST = N_NODE // CH
+DST_P = NODE_IN // 4
+DST_SCALE_P = 34
 REP = 4
 LAST = GT - 1
 Y_BUFS = 8
@@ -48,10 +46,10 @@ FLOPS = 2 * 2 * N_NODE * N_NODE * D_IN * HID
 
 def tile_edge_update_only_pa_t_kernel(tc, node_fts, edge_fts, Wt, out):
     nc = tc.nc
-    edge_v = edge_fts.rearrange("b (c p t) f -> p (b c) (t f)", p=P, t=CH)
-    out_v = out.rearrange("b (c p t) h -> (b c) p t h", p=P, t=CH)
+    edge_v = edge_fts.rearrange("b (i k) f -> (b i) k f", k=N_NODE)
+    out_v = out.rearrange("b (i k) h -> (b i) k h", k=N_NODE)
     node_rows = node_fts.flatten_outer_dims()
-    w_v = Wt.rearrange("(q p r) k -> p q (r k)", p=P, r=2)
+    w_v = Wt.rearrange("(r p) k -> p r k", p=P)
 
     with ExitStack() as ctx:
         const = ctx.enter_context(tc.tile_pool(name="const", bufs=1))
@@ -87,23 +85,28 @@ def tile_edge_update_only_pa_t_kernel(tc, node_fts, edge_fts, Wt, out):
         wq = const.tile([P, HID], U32, name="wq", align_bytes=64)
         wsc = const.tile([P, HID], U8, name="wsc", align_bytes=64)
 
-        def load_weights(q, n):
-            nc.sync.dma_start(
-                out=wsb[:].rearrange("p (q x) -> p q x", q=4)[:, q : q + n, :], in_=w_v[:, q : q + n, :]
-            )
+        wsb3 = wsb[:].rearrange("p (r k) -> p r k", r=8)
+
+        def load_weights(r0, n):
+            rows = slice(r0, r0 + n)
+            nc.sync.dma_start(out=wsb3[:, rows, 0:NODE_IN], in_=w_v[:, rows, NODE_IN : 2 * NODE_IN])
+            nc.sync.dma_start(out=wsb3[:, rows, NODE_IN : 2 * NODE_IN], in_=w_v[:, rows, 0:NODE_IN])
+            nc.sync.dma_start(out=wsb3[:, rows, 2 * NODE_IN :], in_=w_v[:, rows, 2 * NODE_IN :])
 
         def load_edges(x):
             c, n, ec = edges[x]
-            nc.sync.dma_start(out=ec[:].rearrange("p (c x) -> p c x", c=n), in_=edge_v[:, c : c + n, :])
+            nc.sync.dma_start(
+                out=ec[:].rearrange("p (k f) -> p k f", f=EDGE_IN),
+                in_=edge_v[:, c * CH : (c + n) * CH, :],
+            )
 
         nc.sync.dma_start(
             out=nr[:, 0 : 2 * NODE_IN].rearrange("p (s f) -> p s f", s=2),
             in_=node_rows.unsqueeze(1).to_broadcast([P, 2, NODE_IN]),
         )
         load_edges(0)
-        load_weights(0, 1)
-        load_weights(1, 1)
-        load_weights(2, 2)
+        load_weights(0, 4)
+        load_weights(4, 4)
         load_edges(1)
 
         make_identity(nc, ident[:])
@@ -113,51 +116,37 @@ def tile_edge_update_only_pa_t_kernel(tc, node_fts, edge_fts, Wt, out):
         for pt in packs:
             nc.vector.memset(pt[:].bitcast(I32), 0)
 
-        dcodes = npack[:, 0:CODE_B].bitcast(I32).rearrange("p (b t j) -> p b t j", b=2, t=CH)
-        dscales = npack[:, CODE_B:UNIT_B].bitcast(I32).rearrange("p (b t j) -> p b t j", b=2, t=CH)
+        def fill_src(copy, s):
+            for p0 in (64, 32):
+                copy(
+                    out=slots[s][p0 : p0 + 32, :].bitcast(I32).rearrange("p (t w) -> p t w", t=CH),
+                    in_=npack[p0 : p0 + 32, :].bitcast(I32).unsqueeze(1).to_broadcast([32, CH, UNIT_W]),
+                )
 
-        def units(dst, p0, n):
-            return dst[p0 : p0 + n, :].bitcast(I32).rearrange("p (t w) -> p t w", w=UNIT_W)
+        codes_k = npack[0:DST_P, 0:CODE_B].bitcast(I32).rearrange("p (b k) -> p k b", b=2)
+        scales_k = n4s[0:DST_SCALE_P, :].bitcast(I32).rearrange("p (b k) -> p k b", b=2)
 
-        def fill_dst_codes(engine, dst, p0, src):
-            nt = src.shape[1]
-            engine.tensor_copy(
-                out=units(dst, p0, 32)[:, :, 0:CODE_W].rearrange("p t (i j) -> p t i j", j=N_DST),
-                in_=src.unsqueeze(2).to_broadcast([32, nt, N_SRC, N_DST]),
+        def units(g, rows):
+            lo = (g % 2) * GT * UNIT_B
+            st = slots[(g // 2) % N_SLOTS]
+            return st[0:rows, lo : lo + GT * UNIT_B].bitcast(I32).rearrange("p (t w) -> p t w", t=GT)
+
+        def spread_codes(copy, g):
+            copy(
+                out=units(g, DST_P)[:, :, 0:CODE_W].rearrange("p t (b i) -> p t b i", b=2),
+                in_=codes_k[:, g * GT : (g + 1) * GT, :].unsqueeze(3).to_broadcast([DST_P, GT, 2, N_NODE]),
             )
 
-        def fill_dst_scales(engine, dst, p0, src):
-            nt = src.shape[1]
-            engine.tensor_copy(
-                out=units(dst, p0, 32)[:, :, CODE_W:UNIT_W].rearrange("p t (i j) -> p t i j", j=N_DST // 4),
-                in_=src.unsqueeze(2).to_broadcast([32, nt, N_SRC, N_DST // 4]),
+        def spread_scales(copy, g):
+            copy(
+                out=units(g, DST_SCALE_P)[:, :, CODE_W:UNIT_W].rearrange("p t (b i) -> p t b i", b=2),
+                in_=scales_k[:, g * GT : (g + 1) * GT, :].unsqueeze(3).to_broadcast([DST_SCALE_P, GT, 2, SCALE_W // 2]),
             )
 
-        scodes = n4c[:].bitcast(I32).rearrange("p (c i r) -> p c i r", i=N_SRC, r=REP)
-        sscales = n4s[:].bitcast(I32).rearrange("p (c i) -> p c i", i=N_SRC)
-
-        def spread_src(dst, c, nt):
-            spread_src_codes(nc.gpsimd, dst, c, nt)
-            spread_src_scales(nc.gpsimd, dst, c, nt)
-
-        def spread_src_codes(engine, dst, c, nt):
-            engine.tensor_copy(
-                out=units(dst, 0, SRC_P)[:, :, 0:CODE_W].rearrange("p t (i j) -> p t i j", j=N_DST),
-                in_=scodes[0:SRC_P, c, :, 0:1].unsqueeze(1).to_broadcast([SRC_P, nt, N_SRC, N_DST]),
-            )
-
-        def spread_src_scales(engine, dst, c, nt):
-            engine.tensor_copy(
-                out=units(dst, 0, SRC_SCALE_P)[:, :, CODE_W:UNIT_W].rearrange("p t (i j) -> p t i j", j=N_DST // 4),
-                in_=sscales[0:SRC_SCALE_P, c, :].unsqueeze(1).unsqueeze(3).to_broadcast(
-                    [SRC_SCALE_P, nt, N_SRC, N_DST // 4]
-                ),
-            )
-
-        def fill_dst(s, b):
-            for p0 in (32, 64):
-                fill_dst_codes(nc.gpsimd, slots[s], p0, dcodes[p0 : p0 + 32, b, :, :])
-                fill_dst_scales(nc.gpsimd, slots[s], p0, dscales[p0 : p0 + 32, b, :, :])
+        def spread_chunk(copy, c):
+            for g in (2 * c, 2 * c + 1):
+                spread_codes(copy, g)
+                spread_scales(copy, g)
 
         banks = {}
         staged = {}
@@ -224,8 +213,8 @@ def tile_edge_update_only_pa_t_kernel(tc, node_fts, edge_fts, Wt, out):
 
         def evacuate_weights(q):
             nc.scalar.copy(
-                out=wgw[:, q * QUARTER : (q + 1) * QUARTER, :].rearrange("p (m r) e -> p m r e", r=2),
-                in_=wbanks[q][:].rearrange("p (r e m) -> p m r e", r=2, e=2),
+                out=wgw[:, q * QUARTER : (q + 1) * QUARTER, :].rearrange("p (r q) e -> p r q e", r=2),
+                in_=wbanks[q][:].rearrange("p (r e q) -> p r q e", r=2, e=2),
             )
 
         def quantise_weights(q):
@@ -251,15 +240,14 @@ def tile_edge_update_only_pa_t_kernel(tc, node_fts, edge_fts, Wt, out):
         ntp = tpp.tile([P, 512], F32, tag="tp")
         for e in range(2):
             nc.tensor.transpose(ntp[:, e * P : (e + 1) * P], nrw[:, :, e], ident[:])
-        for b in range(2):
-            nc.vector.tensor_copy(
-                out=ntb[:].bitcast(F32).rearrange("p (b t j e) -> p b t j e", b=2, t=CH, e=2)[:, b],
-                in_=ntp[:, 0 : 2 * P].rearrange("p (e b j t) -> p b t j e", e=2, b=2, t=CH)[:, b],
-            )
+        nc.vector.tensor_copy(
+            out=ntb[:].bitcast(F32).rearrange("p (q e) -> p q e", e=2),
+            in_=ntp[:, 0 : 2 * P].rearrange("p (e q) -> p q e", e=2),
+        )
         nc.vector.quantize_mx(
             out=npack[:, 0:CODE_B].bitcast(FP8X4), scales=npack[:, CODE_B:UNIT_B], in_=ntb[:]
         )
-        fill_dst_codes(nc.vector, slots[0], 64, dcodes[64:96, 0, :, :])
+        fill_src(nc.vector.tensor_copy, 0)
 
         transpose_edges(0)
         evacuate_edges(nc.scalar.copy, 0)
@@ -272,25 +260,19 @@ def tile_edge_update_only_pa_t_kernel(tc, node_fts, edge_fts, Wt, out):
         )
         quantise_edges(0)
         move_edges(0)
-        fill_dst_codes(nc.vector, slots[0], 32, dcodes[32:64, 0, :, :])
+        spread_codes(nc.vector.tensor_copy, 0)
         nc.vector.quantize_mx(out=n4c[:].bitcast(FP8X4), scales=n4s[:], in_=ntb4[:])
         for q in range(4):
             transpose_weights(q)
             evacuate_weights(q)
-        quantise_weights(0)
-        for p0 in (64, 32):
-            fill_dst_scales(nc.vector, slots[0], p0, dscales[p0 : p0 + 32, 0, :, :])
-        spread_src_codes(nc.vector, slots[0], 0, CH)
-        spread_src_scales(nc.vector, slots[0], 0, CH)
-        for q in range(1, 4):
+        spread_codes(nc.vector.tensor_copy, 1)
+        for g in range(2):
+            spread_scales(nc.vector.tensor_copy, g)
+        for q in range(4):
             quantise_weights(q)
         transpose_edges(1)
         load_edges(2)
-        for s in (1, 2):
-            for p0 in (64, 32):
-                nc.sync.dma_start(
-                    out=slots[s][p0 : p0 + 32, :].bitcast(I32), in_=slots[0][p0 : p0 + 32, :].bitcast(I32)
-                )
+        fill_src(nc.sync.dma_start, 1)
         for x in range(3, len(edges)):
             load_edges(x)
 
@@ -312,7 +294,12 @@ def tile_edge_update_only_pa_t_kernel(tc, node_fts, edge_fts, Wt, out):
                 ahead = c + 2
             past_vector = not odd and g >= 2
             per_store = 1 if g < 3 or g >= N_GROUPS - 2 else 2
-            order = [natural[-1]] + natural[:-1] if past_vector else natural
+            if g == 0:
+                order = [(0, 0), (1, 0), (0, 1), (1, 1)] + natural[4:]
+            elif past_vector:
+                order = [natural[-1]] + natural[:-1]
+            else:
+                order = natural
             if ahead is not None and g > 0:
                 transpose_edges(ahead)
             seen = set()
@@ -338,19 +325,20 @@ def tile_edge_update_only_pa_t_kernel(tc, node_fts, edge_fts, Wt, out):
                     quantise_edges(ahead)
                     move_edges(ahead)
                     copy_last_edges(ahead)
-                    if N_CHUNKS // 2 <= ahead < N_CHUNKS // 2 + N_SLOTS:
-                        fill_dst(ahead % N_SLOTS, 1)
-                    spread_src(slots[ahead % N_SLOTS], ahead, CH)
+                    if ahead == 2:
+                        fill_src(nc.gpsimd.tensor_copy, 2)
+                    spread_chunk(nc.gpsimd.tensor_copy, ahead)
                 seen.add((t, hf))
                 row = odd * GT + t
                 if g == N_GROUPS - 1 and t == GT - 1:
                     nc.sync.dma_start(
-                        out=out_v[c][:, row : row + 1, hf * HALF : (hf + 1) * HALF], in_=res.unsqueeze(1)
+                        out=out_v[:, c * CH + row : c * CH + row + 1, hf * HALF : (hf + 1) * HALF],
+                        in_=res.unsqueeze(1),
                     )
                     continue
                 t0 = t - t % per_store
                 if all((tt, hh) in seen for tt in range(t0, t0 + per_store) for hh in range(2)):
                     nc.sync.dma_start(
-                        out=out_v[c][:, odd * GT + t0 : odd * GT + t0 + per_store, :],
+                        out=out_v[:, g * GT + t0 : g * GT + t0 + per_store, :],
                         in_=o[:, t0 * HID : (t0 + per_store) * HID].rearrange("p (t h) -> p t h", t=per_store),
                     )

from contextlib import ExitStack

import concourse.mybir as mybir
from concourse.masks import make_identity

F32 = mybir.dt.float32
BF16 = mybir.dt.bfloat16
U32 = mybir.dt.uint32
I32 = mybir.dt.int32
U8 = mybir.dt.uint8
FP8X4 = mybir.dt.float8_e4m3fn_x4
ALU = mybir.AluOpType
ACT = mybir.ActivationFunctionType

P = 128
N_NODE = 64
NODE_IN = 192
EDGE_IN = 128
D_IN = 512
HID = 1024
HALF = 512
QUARTER = 256
GT = 4
N_GROUPS = N_NODE // GT
CH = 8
N_CHUNKS = N_NODE // CH
N_SLOTS = 3
NEG_SLOPE = 0.1
TILE_COLS = 4 * P
TILE_WORDS = EDGE_IN // 2
CODE_B = 4 * P
SCALE_B = P
UNIT_B = CODE_B + SCALE_B
UNIT_W = UNIT_B // 4
CODE_W = CODE_B // 4
SCALE_W = SCALE_B // 4
DST_P = NODE_IN // 4
DST_SCALE_P = 34
REP = 4
LAST = GT - 1
Y_BUFS = 8
FLT_MAX = 3.4028234663852886e38

FLOPS = 2 * 2 * N_NODE * N_NODE * D_IN * HID


def tile_edge_update_only_pa_t_kernel(tc, node_fts, edge_fts, Wt, out):
    nc = tc.nc
    edge_v = edge_fts.rearrange("b (i k) f -> (b i) k f", k=N_NODE)
    out_v = out.rearrange("b (i k) h -> (b i) k h", k=N_NODE)
    node_rows = node_fts.flatten_outer_dims()
    w_v = Wt.rearrange("(r p) k -> p r k", p=P)

    with ExitStack() as ctx:
        const = ctx.enter_context(tc.tile_pool(name="const", bufs=1))
        pkpool = ctx.enter_context(tc.tile_pool(name="pkpool", bufs=3))
        ypool = ctx.enter_context(tc.tile_pool(name="ypool", bufs=Y_BUFS))
        opool = ctx.enter_context(tc.tile_pool(name="opool", bufs=4))
        xpool = ctx.enter_context(tc.tile_pool(name="xpool", bufs=2))
        tpp = ctx.enter_context(tc.psum_pool(name="tpp", bufs=2))
        mxp = ctx.enter_context(tc.psum_pool(name="mxp", bufs=6))
        ctx.enter_context(tc.manual_schedule())

        ident = const.tile([P, P], F32, name="ident")
        nr = const.tile([P, D_IN], BF16, name="nr")
        edges = []
        for c, n in ((0, 1), (1, 1), (2, 2), (4, 2), (6, 2)):
            ec = const.tile([P, n * CH * EDGE_IN], BF16, name="ec%d" % c)
            edges.append((c, n, ec))
        wsb = const.tile([P, 8 * D_IN], BF16, name="wsb")
        npack = const.tile([P, UNIT_B], U8, name="npack", align_bytes=64)
        n4c = const.tile([P, REP * P], U32, name="n4c", align_bytes=64)
        n4s = const.tile([P, REP * P], U8, name="n4s", align_bytes=64)
        ntb = const.tile([P, TILE_COLS], BF16, name="ntb", align_bytes=64)
        ntb4 = const.tile([P, REP * TILE_COLS], BF16, name="ntb4", align_bytes=64)
        packs = []
        for s in range(N_SLOTS):
            pt = const.tile([P, 2 * UNIT_B], U8, name="pack%d" % s, align_bytes=64)
            packs.append(pt)
        slots = []
        for s in range(N_SLOTS):
            st = const.tile([P, CH * UNIT_B], U8, name="st%d" % s, align_bytes=64)
            slots.append(st)
        wg = const.tile([P, 4 * HID], BF16, name="wg", align_bytes=64)
        wq = const.tile([P, HID], U32, name="wq", align_bytes=64)
        wsc = const.tile([P, HID], U8, name="wsc", align_bytes=64)

        wsb3 = wsb[:].rearrange("p (r k) -> p r k", r=8)

        def load_weights(r0, n):
            rows = slice(r0, r0 + n)
            nc.sync.dma_start(out=wsb3[:, rows, 0:NODE_IN], in_=w_v[:, rows, NODE_IN : 2 * NODE_IN])
            nc.sync.dma_start(out=wsb3[:, rows, NODE_IN : 2 * NODE_IN], in_=w_v[:, rows, 0:NODE_IN])
            nc.sync.dma_start(out=wsb3[:, rows, 2 * NODE_IN :], in_=w_v[:, rows, 2 * NODE_IN :])

        def load_edges(x):
            c, n, ec = edges[x]
            nc.sync.dma_start(
                out=ec[:].rearrange("p (k f) -> p k f", f=EDGE_IN),
                in_=edge_v[:, c * CH : (c + n) * CH, :],
            )

        nc.sync.dma_start(
            out=nr[:, 0 : 2 * NODE_IN].rearrange("p (s f) -> p s f", s=2),
            in_=node_rows.unsqueeze(1).to_broadcast([P, 2, NODE_IN]),
        )
        load_edges(0)
        load_weights(0, 4)
        load_weights(4, 4)
        load_edges(1)

        make_identity(nc, ident[:])
        nc.vector.memset(nr[:, 2 * NODE_IN : D_IN], 0.0)
        nc.vector.memset(npack[:, CODE_B:UNIT_B].bitcast(I32), 0)
        nc.vector.memset(n4s[:].bitcast(I32), 0)
        for pt in packs:
            nc.vector.memset(pt[:].bitcast(I32), 0)

        def fill_src(copy, s):
            for p0 in (64, 32):
                copy(
                    out=slots[s][p0 : p0 + 32, :].bitcast(I32).rearrange("p (t w) -> p t w", t=CH),
                    in_=npack[p0 : p0 + 32, :].bitcast(I32).unsqueeze(1).to_broadcast([32, CH, UNIT_W]),
                )

        codes_k = npack[0:DST_P, 0:CODE_B].bitcast(I32).rearrange("p (b k) -> p k b", b=2)
        scales_k = n4s[0:DST_SCALE_P, :].bitcast(I32).rearrange("p (b k) -> p k b", b=2)

        def units(g, rows):
            lo = (g % 2) * GT * UNIT_B
            st = slots[(g // 2) % N_SLOTS]
            return st[0:rows, lo : lo + GT * UNIT_B].bitcast(I32).rearrange("p (t w) -> p t w", t=GT)

        def spread_codes(copy, g):
            copy(
                out=units(g, DST_P)[:, :, 0:CODE_W].rearrange("p t (b i) -> p t b i", b=2),
                in_=codes_k[:, g * GT : (g + 1) * GT, :].unsqueeze(3).to_broadcast([DST_P, GT, 2, N_NODE]),
            )

        def spread_scales(copy, g):
            copy(
                out=units(g, DST_SCALE_P)[:, :, CODE_W:UNIT_W].rearrange("p t (b i) -> p t b i", b=2),
                in_=scales_k[:, g * GT : (g + 1) * GT, :].unsqueeze(3).to_broadcast([DST_SCALE_P, GT, 2, SCALE_W // 2]),
            )

        def spread_chunk(copy, c):
            for g in (2 * c, 2 * c + 1):
                spread_codes(copy, g)
                spread_scales(copy, g)

        banks = {}
        staged = {}

        def transpose_edges(c):
            c0, tile_bf = [(e0, et) for e0, en, et in edges if e0 <= c < e0 + en][0]
            words = tile_bf[:, (c - c0) * CH * EDGE_IN : (c - c0 + 1) * CH * EDGE_IN].bitcast(F32)
            bank = tpp.tile([P, 512], F32, tag="tp")
            for gl in range(2):
                win = words[:, gl * GT * TILE_WORDS : (gl + 1) * GT * TILE_WORDS].rearrange(
                    "p (m e) -> p m e", e=2
                )
                for e in range(2):
                    col = (2 * gl + e) * P
                    nc.tensor.transpose(bank[:, col : col + P], win[:, :, e], ident[:])
            banks[c] = bank

        def evacuate_edges(copier, c):
            pk = pkpool.tile([P, 2 * TILE_COLS], BF16, tag="pk", align_bytes=64)
            copier(
                out=pk[:].bitcast(F32).rearrange("p (g q e) -> p g q e", g=2, e=2),
                in_=banks[c][:].rearrange("p (g e q) -> p g q e", g=2, e=2),
            )
            staged[c] = pk

        def quantise_edges(c):
            pack = packs[c % N_SLOTS]
            for gl in range(2):
                lo = gl * UNIT_B
                nc.vector.quantize_mx(
                    out=pack[:, lo : lo + CODE_B].bitcast(FP8X4),
                    scales=pack[:, lo + CODE_B : lo + UNIT_B],
                    in_=staged[c][:, gl * TILE_COLS : (gl + 1) * TILE_COLS],
                )

        def move_edges(c):
            st = slots[c % N_SLOTS]
            pack = packs[c % N_SLOTS]
            for n in range(GT if c == 0 else LAST):
                nc.sync.dma_start(
                    out=st[96:128, :].bitcast(I32).rearrange("p (g n w) -> p g n w", g=2, n=GT)[:, :, n, :],
                    in_=pack[32 * n : 32 * n + 32, :].bitcast(I32).rearrange("p (g w) -> p g w", g=2),
                )

        def copy_last_edges(c):
            nc.gpsimd.tensor_copy(
                out=slots[c % N_SLOTS][96:128, :]
                .bitcast(U32)
                .rearrange("p (g n w) -> p g n w", g=2, n=GT)[:, :, LAST, :],
                in_=packs[c % N_SLOTS][96:128, :].bitcast(U32).rearrange("p (g w) -> p g w", g=2),
            )

        wsw = wsb[:].bitcast(F32).rearrange("p (r m e) -> p r m e", r=8, e=2)
        wgw = wg[:].bitcast(F32).rearrange("p (h e) -> p h e", e=2)
        wbanks = {}

        def transpose_weights(q):
            wtp = mxp.tile([P, 512], F32, tag="mx")
            for rl in range(2):
                for e in range(2):
                    col = (rl * 2 + e) * P
                    nc.tensor.transpose(wtp[:, col : col + P], wsw[:, 2 * q + rl, :, e], ident[:])
            wbanks[q] = wtp

        def evacuate_weights(q):
            nc.scalar.copy(
                out=wgw[:, q * QUARTER : (q + 1) * QUARTER, :].rearrange("p (r q) e -> p r q e", r=2),
                in_=wbanks[q][:].rearrange("p (r e q) -> p r q e", r=2, e=2),
            )

        def quantise_weights(q):
            cols = slice(q * QUARTER, (q + 1) * QUARTER)
            nc.vector.quantize_mx(
                out=wq[:, cols].bitcast(FP8X4),
                scales=wsc[:, cols],
                in_=wg[:, 4 * q * QUARTER : 4 * (q + 1) * QUARTER],
            )

        def multiply(out_bank, tile_u8, lo, c0, n):
            nc.tensor.matmul_mx(
                out=out_bank,
                lhsT=tile_u8[:, lo : lo + CODE_B].bitcast(FP8X4),
                lhsT_scale=tile_u8[:, lo + CODE_B : lo + UNIT_B],
                rhs=wq[:, c0 : c0 + n].bitcast(FP8X4),
                rhs_scale=wsc[:, c0 : c0 + n],
                start=True,
                stop=True,
            )

        nrw = nr[:].bitcast(F32).rearrange("p (m e) -> p m e", e=2)
        ntp = tpp.tile([P, 512], F32, tag="tp")
        for e in range(2):
            nc.tensor.transpose(ntp[:, e * P : (e + 1) * P], nrw[:, :, e], ident[:])
        nc.vector.tensor_copy(
            out=ntb[:].bitcast(F32).rearrange("p (q e) -> p q e", e=2),
            in_=ntp[:, 0 : 2 * P].rearrange("p (e q) -> p q e", e=2),
        )
        nc.vector.quantize_mx(
            out=npack[:, 0:CODE_B].bitcast(FP8X4), scales=npack[:, CODE_B:UNIT_B], in_=ntb[:]
        )
        fill_src(nc.vector.tensor_copy, 0)

        transpose_edges(0)
        evacuate_edges(nc.scalar.copy, 0)
        nc.scalar.copy(
            out=ntb4[:].bitcast(F32).rearrange("p (q r e) -> p q r e", r=REP, e=2),
            in_=ntp[:, 0 : 2 * P]
            .rearrange("p (e q) -> p q e", e=2)
            .unsqueeze(2)
            .to_broadcast([P, P, REP, 2]),
        )
        quantise_edges(0)
        move_edges(0)
        spread_codes(nc.vector.tensor_copy, 0)
        nc.vector.quantize_mx(out=n4c[:].bitcast(FP8X4), scales=n4s[:], in_=ntb4[:])
        for q in range(4):
            transpose_weights(q)
            evacuate_weights(q)
        spread_codes(nc.vector.tensor_copy, 1)
        for g in range(2):
            spread_scales(nc.vector.tensor_copy, g)
        for q in range(4):
            quantise_weights(q)
        transpose_edges(1)
        load_edges(2)
        fill_src(nc.sync.dma_start, 1)
        for x in range(3, len(edges)):
            load_edges(x)

        def leaky(bank, res):
            y = ypool.tile([P, HALF], F32, tag="y")
            nc.scalar.activation(out=y[:], in_=bank[:], func=ACT.Copy, scale=NEG_SLOPE)
            nc.vector.tensor_tensor(out=res, in0=bank[:], in1=y[:], op=ALU.max)

        natural = [(t, hf) for t in range(GT) for hf in range(2)]
        for g in range(N_GROUPS):
            c = g // 2
            odd = g % 2
            st = slots[c % N_SLOTS]
            o = opool.tile([P, GT * HID], F32, tag="o")
            ahead, copy_at, quantise_at, copier = None, 2, 6, nc.vector.tensor_copy
            if g < 2:
                ahead, copy_at, quantise_at, copier = g + 1, 1, 3, nc.scalar.copy
            elif not odd and c + 2 < N_CHUNKS:
                ahead = c + 2
            past_vector = not odd and g >= 2
            per_store = 1 if g < 3 or g >= N_GROUPS - 2 else 2
            if g == 0:
                order = [(0, 0), (1, 0), (0, 1), (1, 1)] + natural[4:]
            elif past_vector:
                order = [natural[-1]] + natural[:-1]
            else:
                order = natural
            if ahead is not None and g > 0:
                transpose_edges(ahead)
            seen = set()
            for j in range(2 * GT):
                t, hf = order[j]
                mx = mxp.tile([P, HALF], F32, tag="mx")
                multiply(mx[:], st, (odd * GT + t) * UNIT_B, hf * HALF, HALF)
                col = t * HID + hf * HALF
                res = o[:, col : col + HALF]
                if past_vector and j == 0:
                    nc.scalar.copy(out=res, in_=mx[:])
                    x = xpool.tile([P, HALF], F32, tag="x")
                    nc.gpsimd.tensor_scalar(
                        out=x[:], in0=res, scalar1=NEG_SLOPE - 1.0, scalar2=0.0, op0=ALU.mult, op1=ALU.add
                    )
                    nc.gpsimd.tensor_scalar(out=x[:], in0=x[:], scalar1=FLT_MAX, scalar2=0.0, op0=ALU.min, op1=ALU.max)
                    nc.gpsimd.tensor_tensor(out=res, in0=res, in1=x[:], op=ALU.add)
                else:
                    leaky(mx, res)
                if ahead is not None and j == copy_at:
                    evacuate_edges(copier, ahead)
                if ahead is not None and j == quantise_at:
                    quantise_edges(ahead)
                    move_edges(ahead)
                    copy_last_edges(ahead)
                    if ahead == 2:
                        fill_src(nc.gpsimd.tensor_copy, 2)
                    spread_chunk(nc.gpsimd.tensor_copy, ahead)
                seen.add((t, hf))
                row = odd * GT + t
                if g == N_GROUPS - 1 and t == GT - 1:
                    nc.sync.dma_start(
                        out=out_v[:, c * CH + row : c * CH + row + 1, hf * HALF : (hf + 1) * HALF],
                        in_=res.unsqueeze(1),
                    )
                    continue
                t0 = t - t % per_store
                if all((tt, hh) in seen for tt in range(t0, t0 + per_store) for hh in range(2)):
                    nc.sync.dma_start(
                        out=out_v[:, g * GT + t0 : g * GT + t0 + per_store, :],
                        in_=o[:, t0 * HID : (t0 + per_store) * HID].rearrange("p (t h) -> p t h", t=per_store),
                    )
